import numpy as np
import ml_dtypes


def mxq(x, axis, fmt="e4m3"):
    dtype, down = {"e4m3": (ml_dtypes.float8_e4m3fn, 7), "e5m2": (ml_dtypes.float8_e5m2, 14)}[fmt]
    v = np.moveaxis(np.asarray(x, np.float32).astype(ml_dtypes.bfloat16).astype(np.float64), axis, -1)
    blocks = v.reshape(v.shape[:-1] + (-1, 32))
    amax = np.abs(blocks).max(-1, keepdims=True)
    byte = np.maximum(np.where(amax > 0, np.frexp(amax)[1] - 1 + 127, 0) - down, 1)
    scale = np.exp2(byte - 127.0)
    codes = (blocks / scale).astype(np.float32).astype(dtype).astype(np.float64)
    return np.moveaxis((codes * scale).reshape(v.shape), -1, axis)


WIDE = False


def mx_kscale(k):
    if not WIDE:
        return np.ones(k)
    levels = np.array([10, -10, 5, -5, 0])
    a = np.random.permutation(np.resize(levels, k // 512 * 4)).reshape(k // 512, 4)
    idx = np.arange(k)
    return np.exp2(a[idx // 512, idx % 128 // 32])


BF16 = ml_dtypes.bfloat16


def bf(x):
    return np.asarray(x, np.float32).astype(BF16)


def f64(x):
    return np.asarray(x).astype(np.float64)


B, C, H, W, NH = 1, 2048, 16, 32, 4
N = H * W
DH = C // NH
BN_EPS = 1e-5


def signed_gain(n):
    return np.sign(np.random.standard_normal(n)) * (0.6 + 0.8 * np.random.random(n))


def conv_bn(x, w, b, g, beta):
    y = (mxq(f64(w), 1, "e4m3") @ mxq(f64(x).reshape(B, C, N), 1, "e4m3")) + f64(b)[None, :, None]
    return y * (f64(g) / np.sqrt(1.0 + BN_EPS))[None, :, None] + f64(beta)[None, :, None]


def l2norm(t):
    return t / np.maximum(np.sqrt(np.sum(t * t, axis=-1, keepdims=True)), 1e-12)


def setup_inputs():
    s = mx_kscale(C)
    return {"x1": bf(np.random.standard_normal((B, C, H, W)) * s[None, :, None, None]),
            "x2": bf(np.random.standard_normal((B, C, H, W)) * s[None, :, None, None]),
            "k_w": bf(np.random.standard_normal((C, C)) / np.sqrt(C) / s[None, :]),
            "k_b": bf(np.random.standard_normal(C) * 0.15),
            "q_w": bf(np.random.standard_normal((C, C)) / np.sqrt(C) / s[None, :]),
            "q_b": bf(np.random.standard_normal(C) * 0.15),
            "temperature": bf(np.sqrt(N) * (1.0 + 0.2 * np.random.standard_normal((NH, 1, 1)))),
            "bnk_w": bf(signed_gain(C)),
            "bnk_b": bf(np.random.standard_normal(C) * 0.15),
            "bnq_w": bf(signed_gain(C)),
            "bnq_b": bf(np.random.standard_normal(C) * 0.15)}


def reference(x1, x2, k_w, k_b, q_w, q_b, temperature, bnk_w, bnk_b, bnq_w, bnq_b):
    k = l2norm(conv_bn(x1, k_w, k_b, bnk_w, bnk_b).reshape(B, NH, DH, N))
    q = l2norm(conv_bn(x2, q_w, q_b, bnq_w, bnq_b).reshape(B, NH, DH, N))
    return (mxq(q, 3, "e4m3") @ mxq(k, 3, "e4m3").transpose(0, 1, 3, 2)) * f64(temperature)[None]

@@ -1,0 +1,353 @@
+from contextlib import ExitStack
+import math
+
+import concourse.mybir as mybir
+from concourse.masks import make_identity
+
+F32 = mybir.dt.float32
+BF16 = mybir.dt.bfloat16
+U32 = mybir.dt.uint32
+U8 = mybir.dt.uint8
+FP8X4 = mybir.dt.float8_e4m3fn_x4
+ACT = mybir.ActivationFunctionType
+ALU = mybir.AluOpType
+
+P = 128
+WORD = 4
+PAIR = 2
+K_PASS = P * WORD
+
+C = 2048
+N = 512
+HEADS = 4
+DH = C // HEADS
+PASSES = C // K_PASS
+TILES = 2
+ROUNDS_PER_SIDE = C // (TILES * P)
+ROUNDS = 2 * ROUNDS_PER_SIDE
+ROUNDS_PER_HEAD = DH // (TILES * P)
+W_BUFS = 4
+
+BN_SCALE = 1.0 / math.sqrt(1.0 + 1e-5)
+TINY = 1e-24
+
+FLOPS = 2 * 2 * C * C * N + HEADS * 2 * DH * DH * N
+
+
+def tile_transposedattention_fusion_pa_kernel(
+    tc, x1, x2, k_w, k_b, q_w, q_b, temperature, bnk_w, bnk_b, bnq_w, bnq_b, out
+):
+    nc = tc.nc
+
+    x_views = [
+        x.rearrange("b c h w -> (b c) (h w)").rearrange(
+            "(g u p e) n -> g p u (e n)", g=PASSES, u=PAIR, p=P, e=PAIR
+        )
+        for x in (x1, x2)
+    ]
+    w_views = [w.rearrange("(r j p) c -> r p j c", j=TILES, p=P) for w in (k_w, q_w)]
+    out_view = out.rearrange("b h (t p) d -> (b h t) p d", p=P)
+
+    with ExitStack() as ctx:
+        const = ctx.enter_context(tc.tile_pool(name="const", bufs=1))
+        x_raw_pool = ctx.enter_context(tc.tile_pool(name="x_raw", bufs=2 * PASSES))
+        x_grp_pool = ctx.enter_context(tc.tile_pool(name="x_grp", bufs=3))
+        w_raw_pool = ctx.enter_context(tc.tile_pool(name="w_raw", bufs=W_BUFS))
+        w_grp_pool = ctx.enter_context(tc.tile_pool(name="w_grp", bufs=2))
+        w_mx_pool = ctx.enter_context(tc.tile_pool(name="w_mx", bufs=3))
+        small = ctx.enter_context(tc.tile_pool(name="small", bufs=3))
+        rows_pool = ctx.enter_context(tc.tile_pool(name="rows", bufs=3))
+        q_mx_pool = ctx.enter_context(tc.tile_pool(name="q_mx", bufs=3))
+        out_pool = ctx.enter_context(tc.tile_pool(name="out", bufs=4))
+        turn_psum = ctx.enter_context(tc.psum_pool(name="turn", bufs=4))
+        acc_psum = ctx.enter_context(tc.psum_pool(name="acc", bufs=3))
+        score_psum = ctx.enter_context(tc.psum_pool(name="score", bufs=1))
+        ctx.enter_context(tc.manual_schedule())
+
+        ident = const.tile([P, P], F32, name="ident")
+        ident_bf = const.tile([P, P], BF16, name="ident_bf")
+        vec_rows = const.tile([P, P], BF16, name="vec_rows")
+        vec_cols = const.tile([P, P], F32, name="vec_cols")
+        affine = const.tile([P, 2 * C // P, 2], F32, name="affine")
+        temp_bf = const.tile([P, HEADS], BF16, name="temp_bf")
+        temp = const.tile([P, HEADS], F32, name="temp")
+        one = const.tile([P, 1], F32, name="one")
+        one_root = const.tile([P, 1], F32, name="one_root")
+        x_codes = const.tile([P, 2, PASSES, N], U32, name="x_codes", align_bytes=64)
+        x_scales = const.tile([P, 2, PASSES, N], U8, name="x_scales", align_bytes=64)
+        kn_codes = const.tile([P, HEADS, DH], U32, name="kn_codes", align_bytes=64)
+        kn_scales = const.tile([P, HEADS, DH], U8, name="kn_scales", align_bytes=64)
+
+        x_raw, x_grp = {}, {}
+        w_raw, w_grp, w_codes, w_scales = {}, {}, {}, {}
+        acc, sumsq, inv_norm, rows, rows_grp = {}, {}, {}, {}, {}
+        qn_codes, qn_scales = {}, {}
+
+        def in_range(r):
+            return 0 <= r < ROUNDS
+
+        def load_x(side):
+            for g in range(PASSES):
+                raw = x_raw_pool.tile([P, WORD, N], BF16, name="x_raw", tag="x_raw")
+                nc.sync.dma_start(
+                    out=raw[:].rearrange("p (u e) n -> p u (e n)", u=PAIR), in_=x_views[side][g]
+                )
+                x_raw[(side, g)] = raw
+
+        def load_w(r):
+            if not in_range(r):
+                return
+            side, part = divmod(r, ROUNDS_PER_SIDE)
+            raw = w_raw_pool.tile([P, TILES, C], BF16, name="w_raw", tag="w_raw")
+            nc.sync.dma_start(out=raw[:], in_=w_views[side][part])
+            w_raw[r] = raw
+
+        def regroup_x(side, g, copy):
+            if not 0 <= g < PASSES:
+                return
+            grp = x_grp_pool.tile([P, N, WORD], BF16, name="x_grp", tag="x_grp", align_bytes=64)
+            copy(
+                out=grp[:].rearrange("p (c i) t -> p c t i", i=4),
+                in_=x_raw[(side, g)][:].rearrange("p t (c i) -> p c t i", i=4),
+            )
+            x_grp[(side, g)] = grp
+
+        def quantise_x(side, g):
+            if not 0 <= g < PASSES:
+                return
+            nc.vector.quantize_mx(
+                out=x_codes[:, side, g, :].bitcast(FP8X4),
+                scales=x_scales[:, side, g, :],
+                in_=x_grp[(side, g)][:].rearrange("p n t -> p (n t)"),
+            )
+
+        def turn_four(sources, dest, copy):
+            bank = turn_psum.tile([P, 2, PAIR, P], F32, name="bank", tag="bank")
+            for a in range(2):
+                for u in range(PAIR):
+                    nc.tensor.transpose(
+                        out=bank[:, a, u, :], in_=sources[a][:, u * P : (u + 1) * P], identity=ident[:]
+                    )
+            copy(out=dest, in_=bank[:].rearrange("p a u o -> p a o u"))
+
+        def open_weights(r):
+            if not in_range(r):
+                return
+            w_grp[r] = w_grp_pool.tile(
+                [P, TILES, PASSES, P, WORD], BF16, name="w_grp", tag="w_grp", align_bytes=64
+            )
+            w_codes[r] = w_mx_pool.tile(
+                [P, TILES, PASSES, P], U32, name="w_codes", tag="w_codes", align_bytes=64
+            )
+            w_scales[r] = w_mx_pool.tile(
+                [P, TILES, PASSES, P], U8, name="w_scales", tag="w_scales", align_bytes=64
+            )
+
+        def turn_weights(r, b, copy):
+            if not in_range(r):
+                return
+            j, half = divmod(b, 2)
+            words = w_raw[r][:].bitcast(F32)
+            per_pass = K_PASS // PAIR
+            sources = [
+                words[:, j, (2 * half + a) * per_pass : (2 * half + a + 1) * per_pass]
+                for a in range(2)
+            ]
+            turn_four(sources, w_grp[r][:].bitcast(F32)[:, j, 2 * half : 2 * half + 2, :, :], copy)
+
+        def quantise_weights(r, j):
+            if not in_range(r):
+                return
+            nc.vector.quantize_mx(
+                out=w_codes[r][:, j, :, :].rearrange("p g o -> p (g o)").bitcast(FP8X4),
+                scales=w_scales[r][:, j, :, :].rearrange("p g o -> p (g o)"),
+                in_=w_grp[r][:, j, :, :, :].rearrange("p g o t -> p (g o t)"),
+            )
+
+        def project(r, j):
+            if not in_range(r):
+                return
+            side = r // ROUNDS_PER_SIDE
+            bank = acc_psum.tile([P, N], F32, name="acc", tag="acc")
+            for g in range(PASSES):
+                nc.tensor.matmul_mx(
+                    out=bank[:],
+                    lhsT=w_codes[r][:, j, g, :].bitcast(FP8X4),
+                    lhsT_scale=w_scales[r][:, j, g, :],
+                    rhs=x_codes[:, side, g, :].bitcast(FP8X4),
+                    rhs_scale=x_scales[:, side, g, :],
+                    start=(g == 0),
+                    stop=(g == PASSES - 1),
+                )
+            acc[(r, j)] = bank
+
+        def square_sum(r, j):
+            if not in_range(r):
+                return
+            if j == 0:
+                sumsq[r] = small.tile([P, TILES], F32, name="sumsq", tag="sumsq")
+            squares = rows_pool.tile([P, N], BF16, name="squares", tag="squares")
+            tile_no = TILES * r + j
+            nc.scalar.activation(
+                out=squares[:],
+                in_=acc[(r, j)][:],
+                func=ACT.Square,
+                scale=affine[:, tile_no, 0:1],
+                bias=affine[:, tile_no, 1:2],
+                accum_out=sumsq[r][:, j : j + 1],
+            )
+
+        def inverse_norm(r):
+            if not in_range(r):
+                return
+            floored = small.tile([P, TILES], F32, name="floored", tag="floored")
+            inv_sq = small.tile([P, TILES], F32, name="inv_sq", tag="inv_sq")
+            inv_norm[r] = small.tile([P, TILES], F32, name="inv_norm", tag="inv_norm")
+            nc.vector.tensor_scalar_max(out=floored[:], in0=sumsq[r][:], scalar1=TINY)
+            nc.vector.reciprocal(out=inv_sq[:], in_=floored[:])
+            nc.scalar.activation(out=inv_norm[r][:], in_=inv_sq[:], func=ACT.Sqrt)
+
+        def normalise(r):
+            if not in_range(r):
+                return
+            fit = small.tile([P, TILES, 2], F32, name="fit", tag="fit")
+            nc.vector.tensor_tensor(
+                out=fit[:],
+                in0=affine[:, TILES * r : TILES * (r + 1), :],
+                in1=inv_norm[r][:].unsqueeze(2).to_broadcast([P, TILES, 2]),
+                op=ALU.mult,
+            )
+            rows[r] = rows_pool.tile([P, TILES, N], BF16, name="rows", tag="rows")
+            nc.vector.tensor_scalar(
+                out=rows[r][:, 0, :],
+                in0=acc[(r, 0)][:],
+                scalar1=fit[:, 0, 0:1],
+                scalar2=fit[:, 0, 1:2],
+                op0=ALU.mult,
+                op1=ALU.add,
+            )
+            nc.scalar.activation(
+                out=rows[r][:, 1, :],
+                in_=acc[(r, 1)][:],
+                func=ACT.Identity,
+                scale=fit[:, 1, 0:1],
+                bias=fit[:, 1, 1:2],
+            )
+
+        def turn_rows(r, copy):
+            if not in_range(r):
+                return
+            rows_grp[r] = rows_pool.tile(
+                [P, TILES, P, WORD], BF16, name="rows_grp", tag="rows_grp", align_bytes=64
+            )
+            words = rows[r][:].bitcast(F32)
+            turn_four([words[:, j, :] for j in range(TILES)], rows_grp[r][:].bitcast(F32), copy)
+
+        def quantise_rows(r):
+            if not in_range(r):
+                return
+            side, part = divmod(r, ROUNDS_PER_SIDE)
+            head, half = divmod(part, ROUNDS_PER_HEAD)
+            width = TILES * P
+            if side == 0:
+                codes = kn_codes[:, head, half * width : (half + 1) * width]
+                scales = kn_scales[:, head, half * width : (half + 1) * width]
+            else:
+                qn_codes[r] = q_mx_pool.tile([P, width], U32, name="qn_codes", tag="qn_codes", align_bytes=64)
+                qn_scales[r] = q_mx_pool.tile([P, width], U8, name="qn_scales", tag="qn_scales", align_bytes=64)
+                codes, scales = qn_codes[r][:], qn_scales[r][:]
+            nc.vector.quantize_mx(
+                out=codes.bitcast(FP8X4),
+                scales=scales,
+                in_=rows_grp[r][:].rearrange("p j o t -> p (j o t)"),
+            )
+
+        def score(r, j):
+            if not ROUNDS_PER_SIDE <= r < ROUNDS:
+                return
+            part = r - ROUNDS_PER_SIDE
+            head = part // ROUNDS_PER_HEAD
+            bank = score_psum.tile([P, DH], F32, name="score", tag="score")
+            nc.tensor.matmul_mx(
+                out=bank[:],
+                lhsT=qn_codes[r][:, j * P : (j + 1) * P].bitcast(FP8X4),
+                lhsT_scale=qn_scales[r][:, j * P : (j + 1) * P],
+                rhs=kn_codes[:, head, :].bitcast(FP8X4),
+                rhs_scale=kn_scales[:, head, :],
+                start=True,
+                stop=True,
+            )
+            result = out_pool.tile([P, DH], F32, name="result", tag="result")
+            if j == 0:
+                nc.scalar.activation(
+                    out=result[:], in_=bank[:], func=ACT.Copy, scale=temp[:, head : head + 1]
+                )
+            else:
+                nc.vector.tensor_scalar(
+                    out=result[:], in0=bank[:], scalar1=temp[:, head : head + 1], scalar2=None, op0=ALU.mult
+                )
+            nc.sync.dma_start(out=out_view[TILES * part + j], in_=result[:])
+
+        def iteration(r):
+            open_weights(r + 1)
+            turn_weights(r + 1, 0, nc.vector.tensor_copy)
+            turn_weights(r + 1, 1, nc.scalar.copy)
+            inverse_norm(r - 1)
+            turn_weights(r + 1, 2, nc.scalar.copy)
+            normalise(r - 1)
+            turn_weights(r + 1, 3, nc.scalar.copy)
+            load_w(r + 1 + W_BUFS)
+            quantise_weights(r + 1, 0)
+            turn_rows(r - 2, nc.vector.tensor_copy)
+            quantise_weights(r + 1, 1)
+            quantise_rows(r - 2)
+            quantise_x(1, r - 3)
+            regroup_x(1, r - 2, nc.vector.tensor_copy)
+            for j in range(TILES):
+                project(r, j)
+                square_sum(r, j)
+                score(r - 3, j)
+
+        nc.vector.memset(vec_rows[:], 0.0)
+        nc.vector.memset(one[:], 1.0)
+        rows_per_vec = C // P
+        for v, vec in enumerate((k_b, bnk_w, bnk_b, q_b, bnq_w, bnq_b)):
+            nc.scalar.dma_start(
+                out=vec_rows[v * rows_per_vec : (v + 1) * rows_per_vec, :],
+                in_=vec.rearrange("(i p) -> i p", p=P),
+            )
+        nc.scalar.dma_start(
+            out=temp_bf[:], in_=temperature.rearrange("h a b -> (h a b)").partition_broadcast(P)
+        )
+        nc.scalar.activation(out=one_root[:], in_=one[:], func=ACT.Sqrt)
+        make_identity(nc, ident_bf[:])
+        make_identity(nc, ident[:])
+
+        load_x(0)
+        for r in range(W_BUFS):
+            load_w(r)
+        load_x(1)
+
+        vec_bank = score_psum.tile([P, P], BF16, name="vec_bank", tag="score")
+        nc.tensor.transpose(out=vec_bank[:], in_=vec_rows[:], identity=ident_bf[:])
+
+        for g in range(PASSES):
+            regroup_x(0, g, nc.vector.tensor_copy if g % 2 == 0 else nc.scalar.copy)
+            quantise_x(0, g - 1)
+        quantise_x(0, PASSES - 1)
+
+        iteration(-1)
+
+        nc.vector.tensor_copy(out=vec_cols[:], in_=vec_bank[:])
+        nc.vector.tensor_copy(out=temp[:], in_=temp_bf[:])
+        by_vec = vec_cols[:, 0 : 6 * rows_per_vec].rearrange("p (s v i) -> p s v i", s=2, v=3)
+        by_side = affine[:].rearrange("p (s i) c -> p s i c", s=2)
+        gain, shift = by_side[:, :, :, 0], by_side[:, :, :, 1]
+        nc.vector.tensor_scalar(
+            out=gain, in0=by_vec[:, :, 1, :], scalar1=BN_SCALE, scalar2=None, op0=ALU.mult
+        )
+        nc.vector.tensor_tensor(out=shift, in0=by_vec[:, :, 0, :], in1=gain, op=ALU.mult)
+        nc.vector.tensor_tensor(out=shift, in0=shift, in1=by_vec[:, :, 2, :], op=ALU.add)
+
+        for r in range(ROUNDS + 3):
+            iteration(r)

@@ -29,7 +29,9 @@ ROUNDS_PER_HEAD = DH // (TILES * P)
 W_BUFS = 4
 
 BN_SCALE = 1.0 / math.sqrt(1.0 + 1e-5)
-TINY = 1e-24
+MAX_INV_NORM = 1e12
+X_STEPS = 2 * PASSES
+X_STEP_COLS = N // 2
 
 FLOPS = 2 * 2 * C * C * N + HEADS * 2 * DH * DH * N
 
@@ -59,9 +61,8 @@ def tile_transposedattention_fusion_pa_kernel(
         rows_pool = ctx.enter_context(tc.tile_pool(name="rows", bufs=3))
         q_mx_pool = ctx.enter_context(tc.tile_pool(name="q_mx", bufs=3))
         out_pool = ctx.enter_context(tc.tile_pool(name="out", bufs=4))
-        turn_psum = ctx.enter_context(tc.psum_pool(name="turn", bufs=4))
+        bank_psum = ctx.enter_context(tc.psum_pool(name="bank", bufs=5))
         acc_psum = ctx.enter_context(tc.psum_pool(name="acc", bufs=3))
-        score_psum = ctx.enter_context(tc.psum_pool(name="score", bufs=1))
         ctx.enter_context(tc.manual_schedule())
 
         ident = const.tile([P, P], F32, name="ident")
@@ -86,13 +87,12 @@ def tile_transposedattention_fusion_pa_kernel(
         def in_range(r):
             return 0 <= r < ROUNDS
 
-        def load_x(side):
-            for g in range(PASSES):
-                raw = x_raw_pool.tile([P, WORD, N], BF16, name="x_raw", tag="x_raw")
-                nc.sync.dma_start(
-                    out=raw[:].rearrange("p (u e) n -> p u (e n)", u=PAIR), in_=x_views[side][g]
-                )
-                x_raw[(side, g)] = raw
+        def load_x(side, g):
+            raw = x_raw_pool.tile([P, WORD, N], BF16, name="x_raw", tag="x_raw")
+            nc.sync.dma_start(
+                out=raw[:].rearrange("p (u e) n -> p u (e n)", u=PAIR), in_=x_views[side][g]
+            )
+            x_raw[(side, g)] = raw
 
         def load_w(r):
             if not in_range(r):
@@ -102,27 +102,33 @@ def tile_transposedattention_fusion_pa_kernel(
             nc.sync.dma_start(out=raw[:], in_=w_views[side][part])
             w_raw[r] = raw
 
-        def regroup_x(side, g, copy):
-            if not 0 <= g < PASSES:
+        def regroup_x(side, k, copy):
+            if not 0 <= k < X_STEPS:
                 return
-            grp = x_grp_pool.tile([P, N, WORD], BF16, name="x_grp", tag="x_grp", align_bytes=64)
+            g, half = divmod(k, 2)
+            cols = slice(half * X_STEP_COLS, (half + 1) * X_STEP_COLS)
+            grp = x_grp_pool.tile(
+                [P, X_STEP_COLS, WORD], BF16, name="x_grp", tag="x_grp", align_bytes=64
+            )
             copy(
                 out=grp[:].rearrange("p (c i) t -> p c t i", i=4),
-                in_=x_raw[(side, g)][:].rearrange("p t (c i) -> p c t i", i=4),
+                in_=x_raw[(side, g)][:, :, cols].rearrange("p t (c i) -> p c t i", i=4),
             )
-            x_grp[(side, g)] = grp
+            x_grp[(side, k)] = grp
 
-        def quantise_x(side, g):
-            if not 0 <= g < PASSES:
+        def quantise_x(side, k):
+            if not 0 <= k < X_STEPS:
                 return
+            g, half = divmod(k, 2)
+            cols = slice(half * X_STEP_COLS, (half + 1) * X_STEP_COLS)
             nc.vector.quantize_mx(
-                out=x_codes[:, side, g, :].bitcast(FP8X4),
-                scales=x_scales[:, side, g, :],
-                in_=x_grp[(side, g)][:].rearrange("p n t -> p (n t)"),
+                out=x_codes[:, side, g, cols].bitcast(FP8X4),
+                scales=x_scales[:, side, g, cols],
+                in_=x_grp[(side, k)][:].rearrange("p n t -> p (n t)"),
             )
 
         def turn_four(sources, dest, copy):
-            bank = turn_psum.tile([P, 2, PAIR, P], F32, name="bank", tag="bank")
+            bank = bank_psum.tile([P, 2, PAIR, P], F32, name="bank", tag="bank")
             for a in range(2):
                 for u in range(PAIR):
                     nc.tensor.transpose(
@@ -200,22 +206,20 @@ def tile_transposedattention_fusion_pa_kernel(
         def inverse_norm(r):
             if not in_range(r):
                 return
-            floored = small.tile([P, TILES], F32, name="floored", tag="floored")
-            inv_sq = small.tile([P, TILES], F32, name="inv_sq", tag="inv_sq")
             inv_norm[r] = small.tile([P, TILES], F32, name="inv_norm", tag="inv_norm")
-            nc.vector.tensor_scalar_max(out=floored[:], in0=sumsq[r][:], scalar1=TINY)
-            nc.vector.reciprocal(out=inv_sq[:], in_=floored[:])
-            nc.scalar.activation(out=inv_norm[r][:], in_=inv_sq[:], func=ACT.Sqrt)
+            nc.scalar.activation(out=inv_norm[r][:], in_=sumsq[r][:], func=ACT.Abs_reciprocal_sqrt)
 
         def normalise(r):
             if not in_range(r):
                 return
             fit = small.tile([P, TILES, 2], F32, name="fit", tag="fit")
-            nc.vector.tensor_tensor(
+            nc.vector.scalar_tensor_tensor(
                 out=fit[:],
-                in0=affine[:, TILES * r : TILES * (r + 1), :],
-                in1=inv_norm[r][:].unsqueeze(2).to_broadcast([P, TILES, 2]),
-                op=ALU.mult,
+                in0=inv_norm[r][:].unsqueeze(2).to_broadcast([P, TILES, 2]),
+                scalar=MAX_INV_NORM,
+                in1=affine[:, TILES * r : TILES * (r + 1), :],
+                op0=ALU.min,
+                op1=ALU.mult,
             )
             rows[r] = rows_pool.tile([P, TILES, N], BF16, name="rows", tag="rows")
             nc.vector.tensor_scalar(
@@ -267,7 +271,7 @@ def tile_transposedattention_fusion_pa_kernel(
                 return
             part = r - ROUNDS_PER_SIDE
             head = part // ROUNDS_PER_HEAD
-            bank = score_psum.tile([P, DH], F32, name="score", tag="score")
+            bank = bank_psum.tile([P, DH], F32, name="score", tag="bank")
             nc.tensor.matmul_mx(
                 out=bank[:],
                 lhsT=qn_codes[r][:, j * P : (j + 1) * P].bitcast(FP8X4),
@@ -289,24 +293,25 @@ def tile_transposedattention_fusion_pa_kernel(
             nc.sync.dma_start(out=out_view[TILES * part + j], in_=result[:])
 
         def iteration(r):
-            open_weights(r + 1)
-            turn_weights(r + 1, 0, nc.vector.tensor_copy)
-            turn_weights(r + 1, 1, nc.scalar.copy)
+            quantise_weights(r, 1)
             inverse_norm(r - 1)
-            turn_weights(r + 1, 2, nc.scalar.copy)
+            turn_rows(r - 2, nc.vector.tensor_copy)
+            quantise_x(1, r - 1)
+            open_weights(r + 1)
+            turn_weights(r + 1, 0, nc.scalar.copy)
+            turn_weights(r + 1, 1, nc.scalar.copy)
             normalise(r - 1)
+            quantise_rows(r - 2)
+            turn_weights(r + 1, 2, nc.vector.tensor_copy)
             turn_weights(r + 1, 3, nc.scalar.copy)
             load_w(r + 1 + W_BUFS)
+            for j in range(TILES):
+                score(r - 3, j)
             quantise_weights(r + 1, 0)
-            turn_rows(r - 2, nc.vector.tensor_copy)
-            quantise_weights(r + 1, 1)
-            quantise_rows(r - 2)
-            quantise_x(1, r - 3)
-            regroup_x(1, r - 2, nc.vector.tensor_copy)
+            regroup_x(1, r, nc.vector.tensor_copy)
             for j in range(TILES):
                 project(r, j)
                 square_sum(r, j)
-                score(r - 3, j)
 
         nc.vector.memset(vec_rows[:], 0.0)
         nc.vector.memset(one[:], 1.0)
@@ -319,22 +324,26 @@ def tile_transposedattention_fusion_pa_kernel(
         nc.scalar.dma_start(
             out=temp_bf[:], in_=temperature.rearrange("h a b -> (h a b)").partition_broadcast(P)
         )
-        nc.scalar.activation(out=one_root[:], in_=one[:], func=ACT.Sqrt)
+        nc.scalar.activation(out=one_root[:], in_=one[:], func=ACT.Abs_reciprocal_sqrt)
         make_identity(nc, ident_bf[:])
         make_identity(nc, ident[:])
 
-        load_x(0)
-        for r in range(W_BUFS):
+        for g in range(PASSES):
+            load_x(0, g)
+        for r in range(W_BUFS - 1):
             load_w(r)
-        load_x(1)
+        load_x(1, 0)
+        load_w(W_BUFS - 1)
+        for g in range(1, PASSES):
+            load_x(1, g)
 
-        vec_bank = score_psum.tile([P, P], BF16, name="vec_bank", tag="score")
+        vec_bank = bank_psum.tile([P, P], BF16, name="vec_bank", tag="bank")
         nc.tensor.transpose(out=vec_bank[:], in_=vec_rows[:], identity=ident_bf[:])
 
-        for g in range(PASSES):
-            regroup_x(0, g, nc.vector.tensor_copy if g % 2 == 0 else nc.scalar.copy)
-            quantise_x(0, g - 1)
-        quantise_x(0, PASSES - 1)
+        for k in range(X_STEPS):
+            regroup_x(0, k, nc.vector.tensor_copy if k % 2 == 0 else nc.scalar.copy)
+            quantise_x(0, k - 1)
+        quantise_x(0, X_STEPS - 1)
 
         iteration(-1)
 

@@ -67,8 +67,8 @@ def tile_transposedattention_fusion_pa_kernel(
 
         ident = const.tile([P, P], F32, name="ident")
         ident_bf = const.tile([P, P], BF16, name="ident_bf")
-        vec_rows = const.tile([P, P], BF16, name="vec_rows")
-        vec_cols = const.tile([P, P], F32, name="vec_cols")
+        vec_rows = [const.tile([P, P], BF16, name=f"vec_rows_{side}") for side in range(2)]
+        vec_cols = const.tile([P, 2, P], F32, name="vec_cols")
         affine = const.tile([P, 2 * C // P, 2], F32, name="affine")
         temp_bf = const.tile([P, HEADS], BF16, name="temp_bf")
         temp = const.tile([P, HEADS], F32, name="temp")
@@ -99,7 +99,11 @@ def tile_transposedattention_fusion_pa_kernel(
                 return
             side, part = divmod(r, ROUNDS_PER_SIDE)
             raw = w_raw_pool.tile([P, TILES, C], BF16, name="w_raw", tag="w_raw")
-            nc.sync.dma_start(out=raw[:], in_=w_views[side][part])
+            if r == 0:
+                for j in range(TILES):
+                    nc.sync.dma_start(out=raw[:, j, :], in_=w_views[side][part][:, j, :])
+            else:
+                nc.sync.dma_start(out=raw[:], in_=w_views[side][part])
             w_raw[r] = raw
 
         def regroup_x(side, k, copy):
@@ -170,22 +174,25 @@ def tile_transposedattention_fusion_pa_kernel(
                 in_=w_grp[r][:, j, :, :, :].rearrange("p g o t -> p (g o t)"),
             )
 
+        def project_pass(r, j, g):
+            side = r // ROUNDS_PER_SIDE
+            if g == 0:
+                acc[(r, j)] = acc_psum.tile([P, N], F32, name="acc", tag="acc")
+            nc.tensor.matmul_mx(
+                out=acc[(r, j)][:],
+                lhsT=w_codes[r][:, j, g, :].bitcast(FP8X4),
+                lhsT_scale=w_scales[r][:, j, g, :],
+                rhs=x_codes[:, side, g, :].bitcast(FP8X4),
+                rhs_scale=x_scales[:, side, g, :],
+                start=(g == 0),
+                stop=(g == PASSES - 1),
+            )
+
         def project(r, j):
             if not in_range(r):
                 return
-            side = r // ROUNDS_PER_SIDE
-            bank = acc_psum.tile([P, N], F32, name="acc", tag="acc")
             for g in range(PASSES):
-                nc.tensor.matmul_mx(
-                    out=bank[:],
-                    lhsT=w_codes[r][:, j, g, :].bitcast(FP8X4),
-                    lhsT_scale=w_scales[r][:, j, g, :],
-                    rhs=x_codes[:, side, g, :].bitcast(FP8X4),
-                    rhs_scale=x_scales[:, side, g, :],
-                    start=(g == 0),
-                    stop=(g == PASSES - 1),
-                )
-            acc[(r, j)] = bank
+                project_pass(r, j, g)
 
         def square_sum(r, j):
             if not in_range(r):
@@ -293,7 +300,8 @@ def tile_transposedattention_fusion_pa_kernel(
             nc.sync.dma_start(out=out_view[TILES * part + j], in_=result[:])
 
         def iteration(r):
-            quantise_weights(r, 1)
+            if r > 0:
+                quantise_weights(r, 1)
             inverse_norm(r - 1)
             turn_rows(r - 2, nc.vector.tensor_copy)
             quantise_x(1, r - 1)
@@ -309,54 +317,76 @@ def tile_transposedattention_fusion_pa_kernel(
                 score(r - 3, j)
             quantise_weights(r + 1, 0)
             regroup_x(1, r, nc.vector.tensor_copy)
-            for j in range(TILES):
-                project(r, j)
-                square_sum(r, j)
+            if r > 0:
+                for j in range(TILES):
+                    project(r, j)
+                    square_sum(r, j)
 
-        nc.vector.memset(vec_rows[:], 0.0)
-        nc.vector.memset(one[:], 1.0)
         rows_per_vec = C // P
-        for v, vec in enumerate((k_b, bnk_w, bnk_b, q_b, bnq_w, bnq_b)):
-            nc.scalar.dma_start(
-                out=vec_rows[v * rows_per_vec : (v + 1) * rows_per_vec, :],
-                in_=vec.rearrange("(i p) -> i p", p=P),
-            )
-        nc.scalar.dma_start(
-            out=temp_bf[:], in_=temperature.rearrange("h a b -> (h a b)").partition_broadcast(P)
-        )
+
+        def load_vectors(side):
+            for v, vec in enumerate(((k_b, bnk_w, bnk_b), (q_b, bnq_w, bnq_b))[side]):
+                nc.sync.dma_start(
+                    out=vec_rows[side][v * rows_per_vec : (v + 1) * rows_per_vec, :],
+                    in_=vec.rearrange("(i p) -> i p", p=P),
+                )
+
+        def affine_of(side):
+            bank = bank_psum.tile([P, P], BF16, name="vec_bank", tag="bank")
+            nc.tensor.transpose(out=bank[:], in_=vec_rows[side][:], identity=ident_bf[:])
+            cols = vec_cols[:, side, :]
+            nc.vector.tensor_copy(out=cols, in_=bank[:])
+            bias, bn_w, bn_b = [cols[:, v * rows_per_vec : (v + 1) * rows_per_vec] for v in range(3)]
+            mine = affine[:, side * rows_per_vec : (side + 1) * rows_per_vec, :]
+            gain, shift = mine[:, :, 0], mine[:, :, 1]
+            nc.vector.tensor_scalar(out=gain, in0=bn_w, scalar1=BN_SCALE, scalar2=None, op0=ALU.mult)
+            nc.vector.tensor_tensor(out=shift, in0=bias, in1=gain, op=ALU.mult)
+            nc.vector.tensor_tensor(out=shift, in0=shift, in1=bn_b, op=ALU.add)
+
+        nc.vector.memset(one[:], 1.0)
+        for side in range(2):
+            nc.gpsimd.memset(vec_rows[side][:], 0.0)
         nc.scalar.activation(out=one_root[:], in_=one[:], func=ACT.Abs_reciprocal_sqrt)
         make_identity(nc, ident_bf[:])
         make_identity(nc, ident[:])
 
+        load_w(0)
+        load_vectors(0)
         for g in range(PASSES):
             load_x(0, g)
-        for r in range(W_BUFS - 1):
+        for r in range(1, W_BUFS - 1):
             load_w(r)
+        load_vectors(1)
+        nc.sync.dma_start(
+            out=temp_bf[:], in_=temperature.rearrange("h a b -> (h a b)").partition_broadcast(P)
+        )
         load_x(1, 0)
         load_w(W_BUFS - 1)
         for g in range(1, PASSES):
             load_x(1, g)
 
-        vec_bank = bank_psum.tile([P, P], BF16, name="vec_bank", tag="bank")
-        nc.tensor.transpose(out=vec_bank[:], in_=vec_rows[:], identity=ident_bf[:])
-
-        for k in range(X_STEPS):
-            regroup_x(0, k, nc.vector.tensor_copy if k % 2 == 0 else nc.scalar.copy)
-            quantise_x(0, k - 1)
-        quantise_x(0, X_STEPS - 1)
-
-        iteration(-1)
-
-        nc.vector.tensor_copy(out=vec_cols[:], in_=vec_bank[:])
-        nc.vector.tensor_copy(out=temp[:], in_=temp_bf[:])
-        by_vec = vec_cols[:, 0 : 6 * rows_per_vec].rearrange("p (s v i) -> p s v i", s=2, v=3)
-        by_side = affine[:].rearrange("p (s i) c -> p s i c", s=2)
-        gain, shift = by_side[:, :, :, 0], by_side[:, :, :, 1]
-        nc.vector.tensor_scalar(
-            out=gain, in0=by_vec[:, :, 1, :], scalar1=BN_SCALE, scalar2=None, op0=ALU.mult
-        )
-        nc.vector.tensor_tensor(out=shift, in0=by_vec[:, :, 0, :], in1=gain, op=ALU.mult)
-        nc.vector.tensor_tensor(out=shift, in0=shift, in1=by_vec[:, :, 2, :], op=ALU.add)
+        open_weights(0)
+        turn_weights(0, 0, nc.vector.tensor_copy)
+        for b in range(1, 2 * TILES):
+            turn_weights(0, b, nc.scalar.copy)
+        load_w(W_BUFS)
+        quantise_weights(0, 0)
+        regroup_x(0, 0, nc.vector.tensor_copy)
+        regroup_x(0, 1, nc.scalar.copy)
+        quantise_weights(0, 1)
+        affine_of(0)
+        for g in range(PASSES):
+            regroup_x(0, 2 * g + 2, nc.vector.tensor_copy)
+            regroup_x(0, 2 * g + 3, nc.scalar.copy)
+            quantise_x(0, 2 * g)
+            quantise_x(0, 2 * g + 1)
+            for j in range(TILES):
+                project_pass(0, j, g)
+        for j in range(TILES):
+            square_sum(0, j)
 
         for r in range(ROUNDS + 3):
             iteration(r)
+            if r == 1:
+                affine_of(1)
+                nc.vector.tensor_copy(out=temp[:], in_=temp_bf[:])

@@ -32,6 +32,10 @@ BN_SCALE = 1.0 / math.sqrt(1.0 + 1e-5)
 MAX_INV_NORM = 1e12
 X_STEPS = 2 * PASSES
 X_STEP_COLS = N // 2
+ALL_TILES = slice(0, TILES)
+ONE_TILE = [slice(j, j + 1) for j in range(TILES)]
+ALL_PIXELS = slice(0, N)
+HALVES = (slice(0, N // 2), slice(N // 2, N))
 
 FLOPS = 2 * 2 * C * C * N + HEADS * 2 * DH * DH * N
 
@@ -53,14 +57,14 @@ def tile_transposedattention_fusion_pa_kernel(
     with ExitStack() as ctx:
         const = ctx.enter_context(tc.tile_pool(name="const", bufs=1))
         x_raw_pool = ctx.enter_context(tc.tile_pool(name="x_raw", bufs=2 * PASSES))
-        x_grp_pool = ctx.enter_context(tc.tile_pool(name="x_grp", bufs=3))
+        x_grp_pool = ctx.enter_context(tc.tile_pool(name="x_grp", bufs=X_STEPS))
         w_raw_pool = ctx.enter_context(tc.tile_pool(name="w_raw", bufs=W_BUFS))
         w_grp_pool = ctx.enter_context(tc.tile_pool(name="w_grp", bufs=2))
         w_mx_pool = ctx.enter_context(tc.tile_pool(name="w_mx", bufs=3))
         small = ctx.enter_context(tc.tile_pool(name="small", bufs=3))
         rows_pool = ctx.enter_context(tc.tile_pool(name="rows", bufs=3))
         q_mx_pool = ctx.enter_context(tc.tile_pool(name="q_mx", bufs=3))
-        out_pool = ctx.enter_context(tc.tile_pool(name="out", bufs=4))
+        out_pool = ctx.enter_context(tc.tile_pool(name="out", bufs=8))
         bank_psum = ctx.enter_context(tc.psum_pool(name="bank", bufs=5))
         acc_psum = ctx.enter_context(tc.psum_pool(name="acc", bufs=3))
         ctx.enter_context(tc.manual_schedule())
@@ -81,7 +85,7 @@ def tile_transposedattention_fusion_pa_kernel(
 
         x_raw, x_grp = {}, {}
         w_raw, w_grp, w_codes, w_scales = {}, {}, {}, {}
-        acc, sumsq, inv_norm, rows, rows_grp = {}, {}, {}, {}, {}
+        acc, sumsq, inv_norm, fit, rows, rows_grp = {}, {}, {}, {}, {}, {}
         qn_codes, qn_scales = {}, {}
 
         def in_range(r):
@@ -94,17 +98,13 @@ def tile_transposedattention_fusion_pa_kernel(
             )
             x_raw[(side, g)] = raw
 
-        def load_w(r):
+        def load_w(r, tiles=ALL_TILES):
             if not in_range(r):
                 return
             side, part = divmod(r, ROUNDS_PER_SIDE)
-            raw = w_raw_pool.tile([P, TILES, C], BF16, name="w_raw", tag="w_raw")
-            if r == 0:
-                for j in range(TILES):
-                    nc.sync.dma_start(out=raw[:, j, :], in_=w_views[side][part][:, j, :])
-            else:
-                nc.sync.dma_start(out=raw[:], in_=w_views[side][part])
-            w_raw[r] = raw
+            if tiles.start == 0:
+                w_raw[r] = w_raw_pool.tile([P, TILES, C], BF16, name="w_raw", tag="w_raw")
+            nc.sync.dma_start(out=w_raw[r][:, tiles, :], in_=w_views[side][part][:, tiles, :])
 
         def regroup_x(side, k, copy):
             if not 0 <= k < X_STEPS:
@@ -131,13 +131,16 @@ def tile_transposedattention_fusion_pa_kernel(
                 in_=x_grp[(side, k)][:].rearrange("p n t -> p (n t)"),
             )
 
-        def turn_four(sources, dest, copy):
-            bank = bank_psum.tile([P, 2, PAIR, P], F32, name="bank", tag="bank")
-            for a in range(2):
+        def turn(sources):
+            bank = bank_psum.tile([P, len(sources), PAIR, P], F32, name="bank", tag="bank")
+            for a, source in enumerate(sources):
                 for u in range(PAIR):
                     nc.tensor.transpose(
-                        out=bank[:, a, u, :], in_=sources[a][:, u * P : (u + 1) * P], identity=ident[:]
+                        out=bank[:, a, u, :], in_=source[:, u * P : (u + 1) * P], identity=ident[:]
                     )
+            return bank
+
+        def copy_out(bank, dest, copy):
             copy(out=dest, in_=bank[:].rearrange("p a u o -> p a o u"))
 
         def open_weights(r):
@@ -153,17 +156,24 @@ def tile_transposedattention_fusion_pa_kernel(
                 [P, TILES, PASSES, P], U8, name="w_scales", tag="w_scales", align_bytes=64
             )
 
-        def turn_weights(r, b, copy):
-            if not in_range(r):
-                return
+        def turn_weights_in(r, b):
             j, half = divmod(b, 2)
             words = w_raw[r][:].bitcast(F32)
             per_pass = K_PASS // PAIR
-            sources = [
-                words[:, j, (2 * half + a) * per_pass : (2 * half + a + 1) * per_pass]
-                for a in range(2)
-            ]
-            turn_four(sources, w_grp[r][:].bitcast(F32)[:, j, 2 * half : 2 * half + 2, :, :], copy)
+            return turn(
+                [
+                    words[:, j, (2 * half + a) * per_pass : (2 * half + a + 1) * per_pass]
+                    for a in range(2)
+                ]
+            )
+
+        def turn_weights_out(r, b, bank, copy):
+            j, half = divmod(b, 2)
+            copy_out(bank, w_grp[r][:].bitcast(F32)[:, j, 2 * half : 2 * half + 2, :, :], copy)
+
+        def turn_weights(r, b, copy):
+            if in_range(r):
+                turn_weights_out(r, b, turn_weights_in(r, b), copy)
 
         def quantise_weights(r, j):
             if not in_range(r):
@@ -210,51 +220,71 @@ def tile_transposedattention_fusion_pa_kernel(
                 accum_out=sumsq[r][:, j : j + 1],
             )
 
-        def inverse_norm(r):
+        def inverse_norm(r, tiles=ALL_TILES):
             if not in_range(r):
                 return
-            inv_norm[r] = small.tile([P, TILES], F32, name="inv_norm", tag="inv_norm")
-            nc.scalar.activation(out=inv_norm[r][:], in_=sumsq[r][:], func=ACT.Abs_reciprocal_sqrt)
+            if tiles.start == 0:
+                inv_norm[r] = small.tile([P, TILES], F32, name="inv_norm", tag="inv_norm")
+            nc.scalar.activation(
+                out=inv_norm[r][:, tiles], in_=sumsq[r][:, tiles], func=ACT.Abs_reciprocal_sqrt
+            )
+
+        def fold_norm(r, tiles=ALL_TILES):
+            if not in_range(r):
+                return
+            if tiles.start == 0:
+                fit[r] = small.tile([P, TILES, 2], F32, name="fit", tag="fit")
+                rows[r] = rows_pool.tile([P, TILES, N], BF16, name="rows", tag="rows")
+            count = tiles.stop - tiles.start
+            nc.vector.scalar_tensor_tensor(
+                out=fit[r][:, tiles, :],
+                in0=inv_norm[r][:, tiles].unsqueeze(2).to_broadcast([P, count, 2]),
+                scalar=MAX_INV_NORM,
+                in1=affine[:, TILES * r + tiles.start : TILES * r + tiles.stop, :],
+                op0=ALU.min,
+                op1=ALU.mult,
+            )
+
+        def normalise_on_vector(r, j, cols=ALL_PIXELS):
+            nc.vector.tensor_scalar(
+                out=rows[r][:, j, cols],
+                in0=acc[(r, j)][:, cols],
+                scalar1=fit[r][:, j, 0:1],
+                scalar2=fit[r][:, j, 1:2],
+                op0=ALU.mult,
+                op1=ALU.add,
+            )
+
+        def normalise_on_scalar(r, j, cols=ALL_PIXELS):
+            nc.scalar.activation(
+                out=rows[r][:, j, cols],
+                in_=acc[(r, j)][:, cols],
+                func=ACT.Identity,
+                scale=fit[r][:, j, 0:1],
+                bias=fit[r][:, j, 1:2],
+            )
 
         def normalise(r):
             if not in_range(r):
                 return
-            fit = small.tile([P, TILES, 2], F32, name="fit", tag="fit")
-            nc.vector.scalar_tensor_tensor(
-                out=fit[:],
-                in0=inv_norm[r][:].unsqueeze(2).to_broadcast([P, TILES, 2]),
-                scalar=MAX_INV_NORM,
-                in1=affine[:, TILES * r : TILES * (r + 1), :],
-                op0=ALU.min,
-                op1=ALU.mult,
-            )
-            rows[r] = rows_pool.tile([P, TILES, N], BF16, name="rows", tag="rows")
-            nc.vector.tensor_scalar(
-                out=rows[r][:, 0, :],
-                in0=acc[(r, 0)][:],
-                scalar1=fit[:, 0, 0:1],
-                scalar2=fit[:, 0, 1:2],
-                op0=ALU.mult,
-                op1=ALU.add,
-            )
-            nc.scalar.activation(
-                out=rows[r][:, 1, :],
-                in_=acc[(r, 1)][:],
-                func=ACT.Identity,
-                scale=fit[:, 1, 0:1],
-                bias=fit[:, 1, 1:2],
+            fold_norm(r)
+            normalise_on_vector(r, 0)
+            normalise_on_scalar(r, 1)
+
+        def open_rows(r):
+            rows_grp[r] = rows_pool.tile(
+                [P, TILES, P, WORD], BF16, name="rows_grp", tag="rows_grp", align_bytes=64
             )
 
         def turn_rows(r, copy):
             if not in_range(r):
                 return
-            rows_grp[r] = rows_pool.tile(
-                [P, TILES, P, WORD], BF16, name="rows_grp", tag="rows_grp", align_bytes=64
-            )
+            open_rows(r)
             words = rows[r][:].bitcast(F32)
-            turn_four([words[:, j, :] for j in range(TILES)], rows_grp[r][:].bitcast(F32), copy)
+            bank = turn([words[:, j, :] for j in range(TILES)])
+            copy_out(bank, rows_grp[r][:].bitcast(F32), copy)
 
-        def quantise_rows(r):
+        def quantise_rows(r, tiles=ALL_TILES):
             if not in_range(r):
                 return
             side, part = divmod(r, ROUNDS_PER_SIDE)
@@ -264,13 +294,15 @@ def tile_transposedattention_fusion_pa_kernel(
                 codes = kn_codes[:, head, half * width : (half + 1) * width]
                 scales = kn_scales[:, head, half * width : (half + 1) * width]
             else:
-                qn_codes[r] = q_mx_pool.tile([P, width], U32, name="qn_codes", tag="qn_codes", align_bytes=64)
-                qn_scales[r] = q_mx_pool.tile([P, width], U8, name="qn_scales", tag="qn_scales", align_bytes=64)
+                if tiles.start == 0:
+                    qn_codes[r] = q_mx_pool.tile([P, width], U32, name="qn_codes", tag="qn_codes", align_bytes=64)
+                    qn_scales[r] = q_mx_pool.tile([P, width], U8, name="qn_scales", tag="qn_scales", align_bytes=64)
                 codes, scales = qn_codes[r][:], qn_scales[r][:]
+            cols = slice(tiles.start * P, tiles.stop * P)
             nc.vector.quantize_mx(
-                out=codes.bitcast(FP8X4),
-                scales=scales,
-                in_=rows_grp[r][:].rearrange("p j o t -> p (j o t)"),
+                out=codes[:, cols].bitcast(FP8X4),
+                scales=scales[:, cols],
+                in_=rows_grp[r][:, tiles, :, :].rearrange("p j o t -> p (j o t)"),
             )
 
         def score(r, j):
@@ -300,29 +332,31 @@ def tile_transposedattention_fusion_pa_kernel(
             nc.sync.dma_start(out=out_view[TILES * part + j], in_=result[:])
 
         def iteration(r):
-            if r > 0:
-                quantise_weights(r, 1)
-            inverse_norm(r - 1)
+            quantise_weights(r, 1)
+            if r > 1:
+                inverse_norm(r - 1)
             turn_rows(r - 2, nc.vector.tensor_copy)
             quantise_x(1, r - 1)
             open_weights(r + 1)
             turn_weights(r + 1, 0, nc.scalar.copy)
             turn_weights(r + 1, 1, nc.scalar.copy)
-            normalise(r - 1)
+            if r > 1:
+                normalise(r - 1)
             quantise_rows(r - 2)
-            turn_weights(r + 1, 2, nc.vector.tensor_copy)
+            helped = 0 < r < ROUNDS_PER_SIDE and r % 2 == 1
+            turn_weights(r + 1, 2, nc.scalar.copy if helped else nc.vector.tensor_copy)
             turn_weights(r + 1, 3, nc.scalar.copy)
             load_w(r + 1 + W_BUFS)
             for j in range(TILES):
                 score(r - 3, j)
             quantise_weights(r + 1, 0)
             regroup_x(1, r, nc.vector.tensor_copy)
-            if r > 0:
-                for j in range(TILES):
-                    project(r, j)
-                    square_sum(r, j)
+            for j in range(TILES):
+                project(r, j)
+                square_sum(r, j)
 
         rows_per_vec = C // P
+        vec_bank = {}
 
         def load_vectors(side):
             for v, vec in enumerate(((k_b, bnk_w, bnk_b), (q_b, bnq_w, bnq_b))[side]):
@@ -331,11 +365,13 @@ def tile_transposedattention_fusion_pa_kernel(
                     in_=vec.rearrange("(i p) -> i p", p=P),
                 )
 
-        def affine_of(side):
-            bank = bank_psum.tile([P, P], BF16, name="vec_bank", tag="bank")
-            nc.tensor.transpose(out=bank[:], in_=vec_rows[side][:], identity=ident_bf[:])
+        def turn_vectors(side):
+            vec_bank[side] = bank_psum.tile([P, P], BF16, name="vec_bank", tag="bank")
+            nc.tensor.transpose(out=vec_bank[side][:], in_=vec_rows[side][:], identity=ident_bf[:])
+
+        def make_affine(side):
             cols = vec_cols[:, side, :]
-            nc.vector.tensor_copy(out=cols, in_=bank[:])
+            nc.vector.tensor_copy(out=cols, in_=vec_bank[side][:])
             bias, bn_w, bn_b = [cols[:, v * rows_per_vec : (v + 1) * rows_per_vec] for v in range(3)]
             mine = affine[:, side * rows_per_vec : (side + 1) * rows_per_vec, :]
             gain, shift = mine[:, :, 0], mine[:, :, 1]
@@ -350,11 +386,15 @@ def tile_transposedattention_fusion_pa_kernel(
         make_identity(nc, ident_bf[:])
         make_identity(nc, ident[:])
 
-        load_w(0)
+        for tile in ONE_TILE:
+            load_w(0, tile)
         load_vectors(0)
-        for g in range(PASSES):
+        for g in range(PASSES - 1):
             load_x(0, g)
-        for r in range(1, W_BUFS - 1):
+        load_w(1, ONE_TILE[0])
+        load_x(0, PASSES - 1)
+        load_w(1, ONE_TILE[1])
+        for r in range(2, W_BUFS - 1):
             load_w(r)
         load_vectors(1)
         nc.sync.dma_start(
@@ -369,24 +409,40 @@ def tile_transposedattention_fusion_pa_kernel(
         turn_weights(0, 0, nc.vector.tensor_copy)
         for b in range(1, 2 * TILES):
             turn_weights(0, b, nc.scalar.copy)
+        turn_vectors(0)
         load_w(W_BUFS)
         quantise_weights(0, 0)
         regroup_x(0, 0, nc.vector.tensor_copy)
         regroup_x(0, 1, nc.scalar.copy)
         quantise_weights(0, 1)
-        affine_of(0)
+        open_weights(1)
+        w1_banks = []
         for g in range(PASSES):
+            quantise_x(0, 2 * g)
             regroup_x(0, 2 * g + 2, nc.vector.tensor_copy)
             regroup_x(0, 2 * g + 3, nc.scalar.copy)
-            quantise_x(0, 2 * g)
             quantise_x(0, 2 * g + 1)
             for j in range(TILES):
                 project_pass(0, j, g)
-        for j in range(TILES):
-            square_sum(0, j)
+            if g == 1:
+                w1_banks = [turn_weights_in(1, b) for b in range(2)]
+            if g == PASSES - 2:
+                make_affine(0)
+        turn_weights_out(1, 0, w1_banks[0], nc.scalar.copy)
+        turn_weights_out(1, 1, w1_banks[1], nc.vector.tensor_copy)
+        square_sum(0, 0)
+        turn_weights(1, 2, nc.vector.tensor_copy)
+        square_sum(0, 1)
+        inverse_norm(0)
+        quantise_weights(1, 0)
+        turn_weights(1, 3, nc.scalar.copy)
+        normalise(0)
+        load_w(1 + W_BUFS)
+        regroup_x(1, 0, nc.vector.tensor_copy)
 
-        for r in range(ROUNDS + 3):
+        for r in range(1, ROUNDS + 3):
             iteration(r)
             if r == 1:
-                affine_of(1)
+                turn_vectors(1)
+                make_affine(1)
                 nc.vector.tensor_copy(out=temp[:], in_=temp_bf[:])

@@ -28,6 +28,9 @@ ROUNDS = 2 * ROUNDS_PER_SIDE
 ROUNDS_PER_HEAD = DH // (TILES * P)
 W_BUFS = 4
 
+WARM_BEFORE_WEIGHTS = 6
+WARM_BEFORE_X = 3
+
 BN_SCALE = 1.0 / math.sqrt(1.0 + 1e-5)
 MAX_INV_NORM = 1e12
 X_STEPS = 2 * PASSES
@@ -35,6 +38,7 @@ X_STEP_COLS = N // 2
 ALL_TILES = slice(0, TILES)
 ONE_TILE = [slice(j, j + 1) for j in range(TILES)]
 ALL_PIXELS = slice(0, N)
+ALL_SCORES = slice(0, DH)
 HALVES = (slice(0, N // 2), slice(N // 2, N))
 
 FLOPS = 2 * 2 * C * C * N + HEADS * 2 * DH * DH * N
@@ -78,6 +82,7 @@ def tile_transposedattention_fusion_pa_kernel(
         temp = const.tile([P, HEADS], F32, name="temp")
         one = const.tile([P, 1], F32, name="one")
         one_root = const.tile([P, 1], F32, name="one_root")
+        warm = const.tile([P, N], BF16, name="warm")
         x_codes = const.tile([P, 2, PASSES, N], U32, name="x_codes", align_bytes=64)
         x_scales = const.tile([P, 2, PASSES, N], U8, name="x_scales", align_bytes=64)
         kn_codes = const.tile([P, HEADS, DH], U32, name="kn_codes", align_bytes=64)
@@ -86,7 +91,7 @@ def tile_transposedattention_fusion_pa_kernel(
         x_raw, x_grp = {}, {}
         w_raw, w_grp, w_codes, w_scales = {}, {}, {}, {}
         acc, sumsq, inv_norm, fit, rows, rows_grp = {}, {}, {}, {}, {}, {}
-        qn_codes, qn_scales = {}, {}
+        qn_codes, qn_scales, scores = {}, {}, {}
 
         def in_range(r):
             return 0 <= r < ROUNDS
@@ -276,13 +281,14 @@ def tile_transposedattention_fusion_pa_kernel(
                 [P, TILES, P, WORD], BF16, name="rows_grp", tag="rows_grp", align_bytes=64
             )
 
-        def turn_rows(r, copy):
+        def turn_rows(r, copy, tiles=ALL_TILES):
             if not in_range(r):
                 return
-            open_rows(r)
+            if tiles.start == 0:
+                open_rows(r)
             words = rows[r][:].bitcast(F32)
-            bank = turn([words[:, j, :] for j in range(TILES)])
-            copy_out(bank, rows_grp[r][:].bitcast(F32), copy)
+            bank = turn([words[:, j, :] for j in range(tiles.start, tiles.stop)])
+            copy_out(bank, rows_grp[r][:].bitcast(F32)[:, tiles, :, :], copy)
 
         def quantise_rows(r, tiles=ALL_TILES):
             if not in_range(r):
@@ -320,37 +326,51 @@ def tile_transposedattention_fusion_pa_kernel(
                 start=True,
                 stop=True,
             )
-            result = out_pool.tile([P, DH], F32, name="result", tag="result")
-            if j == 0:
-                nc.scalar.activation(
-                    out=result[:], in_=bank[:], func=ACT.Copy, scale=temp[:, head : head + 1]
-                )
+            scores[(r, j)] = bank
+
+        def scale_scores(r, j, engine, cols=ALL_SCORES):
+            if not ROUNDS_PER_SIDE <= r < ROUNDS:
+                return
+            part = r - ROUNDS_PER_SIDE
+            factor = temp[:, part // ROUNDS_PER_HEAD : part // ROUNDS_PER_HEAD + 1]
+            bank = scores[(r, j)]
+            result = out_pool.tile([P, cols.stop - cols.start], F32, name="result", tag="result")
+            if engine is nc.scalar:
+                nc.scalar.activation(out=result[:], in_=bank[:, cols], func=ACT.Copy, scale=factor)
             else:
                 nc.vector.tensor_scalar(
-                    out=result[:], in0=bank[:], scalar1=temp[:, head : head + 1], scalar2=None, op0=ALU.mult
+                    out=result[:], in0=bank[:, cols], scalar1=factor, scalar2=None, op0=ALU.mult
                 )
-            nc.sync.dma_start(out=out_view[TILES * part + j], in_=result[:])
+            nc.sync.dma_start(out=out_view[TILES * part + j][:, cols], in_=result[:])
+
+        def x2_steps(r):
+            return range(3 * (r - 2) // 2, 3 * (r - 1) // 2) if 2 <= r < ROUNDS_PER_SIDE else ()
 
         def iteration(r):
             quantise_weights(r, 1)
             if r > 1:
                 inverse_norm(r - 1)
             turn_rows(r - 2, nc.vector.tensor_copy)
-            quantise_x(1, r - 1)
+            for k in x2_steps(r - 1):
+                quantise_x(1, k)
             open_weights(r + 1)
             turn_weights(r + 1, 0, nc.scalar.copy)
             turn_weights(r + 1, 1, nc.scalar.copy)
             if r > 1:
                 normalise(r - 1)
             quantise_rows(r - 2)
-            helped = 0 < r < ROUNDS_PER_SIDE and r % 2 == 1
+            helped = r < ROUNDS_PER_SIDE and r % 2 == 1
             turn_weights(r + 1, 2, nc.scalar.copy if helped else nc.vector.tensor_copy)
             turn_weights(r + 1, 3, nc.scalar.copy)
             load_w(r + 1 + W_BUFS)
+            if r == 1:
+                load_x(1, 3)
             for j in range(TILES):
                 score(r - 3, j)
+                scale_scores(r - 3, j, (nc.scalar, nc.vector)[j])
             quantise_weights(r + 1, 0)
-            regroup_x(1, r, nc.vector.tensor_copy)
+            for k in x2_steps(r):
+                regroup_x(1, k, nc.vector.tensor_copy)
             for j in range(TILES):
                 project(r, j)
                 square_sum(r, j)
@@ -371,14 +391,15 @@ def tile_transposedattention_fusion_pa_kernel(
 
         def make_affine(side):
             cols = vec_cols[:, side, :]
-            nc.vector.tensor_copy(out=cols, in_=vec_bank[side][:])
+            nc.scalar.copy(out=cols, in_=vec_bank[side][:])
             bias, bn_w, bn_b = [cols[:, v * rows_per_vec : (v + 1) * rows_per_vec] for v in range(3)]
             mine = affine[:, side * rows_per_vec : (side + 1) * rows_per_vec, :]
             gain, shift = mine[:, :, 0], mine[:, :, 1]
-            nc.vector.tensor_scalar(out=gain, in0=bn_w, scalar1=BN_SCALE, scalar2=None, op0=ALU.mult)
-            nc.vector.tensor_tensor(out=shift, in0=bias, in1=gain, op=ALU.mult)
-            nc.vector.tensor_tensor(out=shift, in0=shift, in1=bn_b, op=ALU.add)
+            nc.gpsimd.tensor_scalar(out=gain, in0=bn_w, scalar1=BN_SCALE, scalar2=None, op0=ALU.mult)
+            nc.gpsimd.tensor_tensor(out=shift, in0=bias, in1=gain, op=ALU.mult)
+            nc.gpsimd.tensor_tensor(out=shift, in0=shift, in1=bn_b, op=ALU.add)
 
+        nc.vector.memset(warm[:], 0.0)
         nc.vector.memset(one[:], 1.0)
         for side in range(2):
             nc.gpsimd.memset(vec_rows[side][:], 0.0)
@@ -386,49 +407,69 @@ def tile_transposedattention_fusion_pa_kernel(
         make_identity(nc, ident_bf[:])
         make_identity(nc, ident[:])
 
-        for tile in ONE_TILE:
-            load_w(0, tile)
+        load_x(0, 0)
+        load_w(0, ONE_TILE[0])
+        load_x(0, 1)
+        load_w(0, ONE_TILE[1])
+        load_x(0, 2)
         load_vectors(0)
-        for g in range(PASSES - 1):
-            load_x(0, g)
-        load_w(1, ONE_TILE[0])
-        load_x(0, PASSES - 1)
-        load_w(1, ONE_TILE[1])
-        for r in range(2, W_BUFS - 1):
-            load_w(r)
+        load_x(0, 3)
+        for tile in ONE_TILE:
+            load_w(1, tile)
+        load_w(2)
         load_vectors(1)
         nc.sync.dma_start(
             out=temp_bf[:], in_=temperature.rearrange("h a b -> (h a b)").partition_broadcast(P)
         )
         load_x(1, 0)
         load_w(W_BUFS - 1)
-        for g in range(1, PASSES):
-            load_x(1, g)
 
+        warm_bank = acc_psum.tile([P, N], F32, name="warm_bank", tag="acc")
+
+        def warm_up(count):
+            for n in range(count):
+                nc.tensor.matmul(out=warm_bank[:], lhsT=warm[:, 0:P], rhs=warm[:], start=True, stop=True)
+
+        warm_up(WARM_BEFORE_WEIGHTS)
         open_weights(0)
-        turn_weights(0, 0, nc.vector.tensor_copy)
-        for b in range(1, 2 * TILES):
-            turn_weights(0, b, nc.scalar.copy)
-        turn_vectors(0)
-        load_w(W_BUFS)
-        quantise_weights(0, 0)
+        open_weights(1)
         regroup_x(0, 0, nc.vector.tensor_copy)
         regroup_x(0, 1, nc.scalar.copy)
+        quantise_x(0, 0)
+        quantise_x(0, 1)
+        turn_weights(0, 0, nc.scalar.copy)
+        turn_weights(0, 1, nc.vector.tensor_copy)
+        warm_up(WARM_BEFORE_X)
+        regroup_x(0, 2, nc.vector.tensor_copy)
+        regroup_x(0, 3, nc.scalar.copy)
+        quantise_weights(0, 0)
+        turn_weights(0, 2, nc.scalar.copy)
+        turn_weights(0, 3, nc.scalar.copy)
+        load_w(W_BUFS)
+        load_x(1, 1)
+        quantise_x(0, 2)
+        quantise_x(0, 3)
+        for g in range(2):
+            project_pass(0, 0, g)
+        regroup_x(0, 4, nc.vector.tensor_copy)
+        regroup_x(0, 5, nc.scalar.copy)
         quantise_weights(0, 1)
-        open_weights(1)
-        w1_banks = []
-        for g in range(PASSES):
-            quantise_x(0, 2 * g)
-            regroup_x(0, 2 * g + 2, nc.vector.tensor_copy)
-            regroup_x(0, 2 * g + 3, nc.scalar.copy)
-            quantise_x(0, 2 * g + 1)
-            for j in range(TILES):
-                project_pass(0, j, g)
-            if g == 1:
-                w1_banks = [turn_weights_in(1, b) for b in range(2)]
-            if g == PASSES - 2:
-                make_affine(0)
+        for g in range(2):
+            project_pass(0, 1, g)
+        turn_vectors(0)
+        quantise_x(0, 4)
+        regroup_x(0, 6, nc.vector.tensor_copy)
+        regroup_x(0, 7, nc.scalar.copy)
+        quantise_x(0, 5)
+        w1_banks = [turn_weights_in(1, b) for b in range(2)]
+        for j in range(TILES):
+            project_pass(0, j, 2)
+        quantise_x(0, 6)
+        quantise_x(0, 7)
+        make_affine(0)
         turn_weights_out(1, 0, w1_banks[0], nc.scalar.copy)
+        for j in range(TILES):
+            project_pass(0, j, 3)
         turn_weights_out(1, 1, w1_banks[1], nc.vector.tensor_copy)
         square_sum(0, 0)
         turn_weights(1, 2, nc.vector.tensor_copy)
@@ -438,11 +479,47 @@ def tile_transposedattention_fusion_pa_kernel(
         turn_weights(1, 3, nc.scalar.copy)
         normalise(0)
         load_w(1 + W_BUFS)
-        regroup_x(1, 0, nc.vector.tensor_copy)
+        load_x(1, 2)
 
-        for r in range(1, ROUNDS + 3):
+        for r in range(1, ROUNDS - 1):
             iteration(r)
             if r == 1:
                 turn_vectors(1)
                 make_affine(1)
                 nc.vector.tensor_copy(out=temp[:], in_=temp_bf[:])
+
+        last = ROUNDS - 1
+        first, second = ONE_TILE
+        quantise_weights(last, 1)
+        inverse_norm(last - 1)
+        turn_rows(last - 2, nc.vector.tensor_copy)
+        normalise(last - 1)
+        for j in range(TILES):
+            score(last - 3, j)
+        scale_scores(last - 3, 0, nc.scalar)
+        scale_scores(last - 3, 1, nc.vector)
+        project(last, 0)
+        square_sum(last, 0)
+        inverse_norm(last, first)
+        quantise_rows(last - 2)
+        project(last, 1)
+        fold_norm(last, first)
+        normalise_on_vector(last, 0)
+        square_sum(last, 1)
+        inverse_norm(last, second)
+        turn_rows(last - 1, nc.scalar.copy)
+        for j in range(TILES):
+            score(last - 2, j)
+        fold_norm(last, second)
+        normalise_on_vector(last, 1)
+        scale_scores(last - 2, 0, nc.scalar)
+        scale_scores(last - 2, 1, nc.scalar)
+        quantise_rows(last - 1)
+        turn_rows(last, nc.vector.tensor_copy, first)
+        turn_rows(last, nc.vector.tensor_copy, second)
+        quantise_rows(last)
+        for r in (last - 1, last):
+            for j in range(TILES):
+                score(r, j)
+            scale_scores(r, 0, nc.scalar)
+            scale_scores(r, 1, nc.vector)

@@ -272,7 +272,6 @@ def tile_transposedattention_fusion_pa_kernel(
         def normalise(r):
             if not in_range(r):
                 return
-            fold_norm(r)
             normalise_on_vector(r, 0)
             normalise_on_scalar(r, 1)
 
@@ -357,8 +356,10 @@ def tile_transposedattention_fusion_pa_kernel(
             turn_weights(r + 1, 0, nc.scalar.copy)
             turn_weights(r + 1, 1, nc.scalar.copy)
             if r > 1:
-                normalise(r - 1)
+                fold_norm(r - 1)
             quantise_rows(r - 2)
+            if r > 1:
+                normalise(r - 1)
             helped = r < ROUNDS_PER_SIDE and r % 2 == 1
             turn_weights(r + 1, 2, nc.scalar.copy if helped else nc.vector.tensor_copy)
             turn_weights(r + 1, 3, nc.scalar.copy)
@@ -477,6 +478,7 @@ def tile_transposedattention_fusion_pa_kernel(
         inverse_norm(0)
         quantise_weights(1, 0)
         turn_weights(1, 3, nc.scalar.copy)
+        fold_norm(0)
         normalise(0)
         load_w(1 + W_BUFS)
         load_x(1, 2)
@@ -493,6 +495,7 @@ def tile_transposedattention_fusion_pa_kernel(
         quantise_weights(last, 1)
         inverse_norm(last - 1)
         turn_rows(last - 2, nc.vector.tensor_copy)
+        fold_norm(last - 1)
         normalise(last - 1)
         for j in range(TILES):
             score(last - 3, j)

@@ -360,7 +360,7 @@ def tile_transposedattention_fusion_pa_kernel(
             quantise_rows(r - 2)
             if r > 1:
                 normalise(r - 1)
-            helped = r < ROUNDS_PER_SIDE and r % 2 == 1
+            helped = 1 < r < ROUNDS_PER_SIDE
             turn_weights(r + 1, 2, nc.scalar.copy if helped else nc.vector.tensor_copy)
             turn_weights(r + 1, 3, nc.scalar.copy)
             load_w(r + 1 + W_BUFS)
@@ -415,9 +415,9 @@ def tile_transposedattention_fusion_pa_kernel(
         load_x(0, 2)
         load_vectors(0)
         load_x(0, 3)
-        for tile in ONE_TILE:
-            load_w(1, tile)
-        load_w(2)
+        for r in (1, 2):
+            for tile in ONE_TILE:
+                load_w(r, tile)
         load_vectors(1)
         nc.sync.dma_start(
             out=temp_bf[:], in_=temperature.rearrange("h a b -> (h a b)").partition_broadcast(P)

@@ -33,6 +33,7 @@ WARM_BEFORE_X = 3
 
 BN_SCALE = 1.0 / math.sqrt(1.0 + 1e-5)
 MAX_INV_NORM = 1e12
+SCALE_PAD = 128
 X_STEPS = 2 * PASSES
 X_STEP_COLS = N // 2
 ALL_TILES = slice(0, TILES)
@@ -83,8 +84,11 @@ def tile_transposedattention_fusion_pa_kernel(
         one = const.tile([P, 1], F32, name="one")
         one_root = const.tile([P, 1], F32, name="one_root")
         warm = const.tile([P, N], BF16, name="warm")
-        x_codes = const.tile([P, 2, PASSES, N], U32, name="x_codes", align_bytes=64)
-        x_scales = const.tile([P, 2, PASSES, N], U8, name="x_scales", align_bytes=64)
+        x_codes = const.tile([P, 2, PASSES, N], U32, name="x_codes", align_bytes=256)
+        x_scales_padded = const.tile(
+            [P, SCALE_PAD + 2 * PASSES * N], U8, name="x_scales", align_bytes=256
+        )
+        x_scales = x_scales_padded[:, SCALE_PAD:].rearrange("p (s g n) -> p s g n", s=2, g=PASSES)
         kn_codes = const.tile([P, HEADS, DH], U32, name="kn_codes", align_bytes=64)
         kn_scales = const.tile([P, HEADS, DH], U8, name="kn_scales", align_bytes=64)
 

@@ -354,19 +354,25 @@ def tile_transposedattention_fusion_pa_kernel(
             if r > 1:
                 inverse_norm(r - 1)
             turn_rows(r - 2, nc.vector.tensor_copy)
-            for k in x2_steps(r - 1):
-                quantise_x(1, k)
             open_weights(r + 1)
             turn_weights(r + 1, 0, nc.scalar.copy)
             turn_weights(r + 1, 1, nc.scalar.copy)
             if r > 1:
                 fold_norm(r - 1)
-            quantise_rows(r - 2)
+            x2_ready = x2_steps(r - 1)
+            for k in x2_ready:
+                quantise_x(1, k)
+            if not x2_ready:
+                quantise_rows(r - 2)
             if r > 1:
-                normalise(r - 1)
+                normalise_on_vector(r - 1, 0)
+            if x2_ready:
+                quantise_rows(r - 2)
             helped = 1 < r < ROUNDS_PER_SIDE
             turn_weights(r + 1, 2, nc.scalar.copy if helped else nc.vector.tensor_copy)
             turn_weights(r + 1, 3, nc.scalar.copy)
+            if r > 1:
+                normalise_on_scalar(r - 1, 1)
             load_w(r + 1 + W_BUFS)
             if r == 1:
                 load_x(1, 3)

@@ -140,8 +140,9 @@ def tile_transposedattention_fusion_pa_kernel(
                 in_=x_grp[(side, k)][:].rearrange("p n t -> p (n t)"),
             )
 
-        def turn(sources):
-            bank = bank_psum.tile([P, len(sources), PAIR, P], F32, name="bank", tag="bank")
+        def turn(sources, pool=None):
+            tag = "bank" if pool is None else "acc"
+            bank = (pool or bank_psum).tile([P, len(sources), PAIR, P], F32, name="bank", tag=tag)
             for a, source in enumerate(sources):
                 for u in range(PAIR):
                     nc.tensor.transpose(
@@ -212,6 +213,21 @@ def tile_transposedattention_fusion_pa_kernel(
                 return
             for g in range(PASSES):
                 project_pass(r, j, g)
+
+        def project_half(r, j, half):
+            side = r // ROUNDS_PER_SIDE
+            cols = HALVES[half]
+            acc[(r, j, half)] = acc_psum.tile([P, N // 2], F32, name="acc_half", tag="acc")
+            for g in range(PASSES):
+                nc.tensor.matmul_mx(
+                    out=acc[(r, j, half)][:],
+                    lhsT=w_codes[r][:, j, g, :].bitcast(FP8X4),
+                    lhsT_scale=w_scales[r][:, j, g, :],
+                    rhs=x_codes[:, side, g, cols].bitcast(FP8X4),
+                    rhs_scale=x_scales[:, side, g, cols],
+                    start=(g == 0),
+                    stop=(g == PASSES - 1),
+                )
 
         def square_sum(r, j):
             if not in_range(r):
@@ -284,13 +300,13 @@ def tile_transposedattention_fusion_pa_kernel(
                 [P, TILES, P, WORD], BF16, name="rows_grp", tag="rows_grp", align_bytes=64
             )
 
-        def turn_rows(r, copy, tiles=ALL_TILES):
+        def turn_rows(r, copy, tiles=ALL_TILES, pool=None):
             if not in_range(r):
                 return
             if tiles.start == 0:
                 open_rows(r)
             words = rows[r][:].bitcast(F32)
-            bank = turn([words[:, j, :] for j in range(tiles.start, tiles.stop)])
+            bank = turn([words[:, j, :] for j in range(tiles.start, tiles.stop)], pool)
             copy_out(bank, rows_grp[r][:].bitcast(F32)[:, tiles, :, :], copy)
 
         def quantise_rows(r, tiles=ALL_TILES):
@@ -345,6 +361,31 @@ def tile_transposedattention_fusion_pa_kernel(
                     out=result[:], in0=bank[:, cols], scalar1=factor, scalar2=None, op0=ALU.mult
                 )
             nc.sync.dma_start(out=out_view[TILES * part + j][:, cols], in_=result[:])
+
+        def score_half(r, j, half):
+            head = (r - ROUNDS_PER_SIDE) // ROUNDS_PER_HEAD
+            bank = bank_psum.tile([P, DH // 2], F32, name="score_half", tag="bank")
+            nc.tensor.matmul_mx(
+                out=bank[:],
+                lhsT=qn_codes[r][:, j * P : (j + 1) * P].bitcast(FP8X4),
+                lhsT_scale=qn_scales[r][:, j * P : (j + 1) * P],
+                rhs=kn_codes[:, head, HALVES[half]].bitcast(FP8X4),
+                rhs_scale=kn_scales[:, head, HALVES[half]],
+                start=True,
+                stop=True,
+            )
+            scores[(r, j, half)] = bank
+
+        def scale_half(r, j, half, engine):
+            part = r - ROUNDS_PER_SIDE
+            factor = temp[:, part // ROUNDS_PER_HEAD : part // ROUNDS_PER_HEAD + 1]
+            bank = scores[(r, j, half)]
+            result = out_pool.tile([P, DH // 2], F32, name="result", tag="result")
+            if engine is nc.scalar:
+                nc.scalar.activation(out=result[:], in_=bank[:], func=ACT.Copy, scale=factor)
+            else:
+                nc.vector.tensor_scalar(out=result[:], in0=bank[:], scalar1=factor, scalar2=None, op0=ALU.mult)
+            nc.sync.dma_start(out=out_view[TILES * part + j][:, HALVES[half]], in_=result[:])
 
         def x2_steps(r):
             return range(3 * (r - 2) // 2, 3 * (r - 1) // 2) if 2 <= r < ROUNDS_PER_SIDE else ()
@@ -502,37 +543,65 @@ def tile_transposedattention_fusion_pa_kernel(
 
         last = ROUNDS - 1
         first, second = ONE_TILE
+        on_vector, on_scalar = nc.vector.tensor_copy, nc.scalar.copy
         quantise_weights(last, 1)
         inverse_norm(last - 1)
-        turn_rows(last - 2, nc.vector.tensor_copy)
+        turn_rows(last - 2, on_vector)
         fold_norm(last - 1)
+        quantise_rows(last - 2)
         normalise(last - 1)
         for j in range(TILES):
             score(last - 3, j)
         scale_scores(last - 3, 0, nc.scalar)
-        scale_scores(last - 3, 1, nc.vector)
         project(last, 0)
+        score(last - 2, 0)
         square_sum(last, 0)
+        scale_scores(last - 3, 1, nc.vector)
         inverse_norm(last, first)
-        quantise_rows(last - 2)
-        project(last, 1)
+        turn_rows(last - 1, on_vector)
+        for half in range(2):
+            project_half(last, 1, half)
         fold_norm(last, first)
-        normalise_on_vector(last, 0)
-        square_sum(last, 1)
-        inverse_norm(last, second)
-        turn_rows(last - 1, nc.scalar.copy)
-        for j in range(TILES):
-            score(last - 2, j)
-        fold_norm(last, second)
-        normalise_on_vector(last, 1)
         scale_scores(last - 2, 0, nc.scalar)
-        scale_scores(last - 2, 1, nc.scalar)
         quantise_rows(last - 1)
-        turn_rows(last, nc.vector.tensor_copy, first)
-        turn_rows(last, nc.vector.tensor_copy, second)
-        quantise_rows(last)
-        for r in (last - 1, last):
-            for j in range(TILES):
-                score(r, j)
-            scale_scores(r, 0, nc.scalar)
-            scale_scores(r, 1, nc.vector)
+        normalise_on_vector(last, 0)
+        half_sums = small.tile([P, 2], F32, name="half_sums")
+        tile_no = TILES * last + 1
+        for half in range(2):
+            squares = rows_pool.tile([P, N], BF16, name="squares", tag="squares")
+            nc.scalar.activation(
+                out=squares[:, HALVES[half]],
+                in_=acc[(last, 1, half)][:],
+                func=ACT.Square,
+                scale=affine[:, tile_no, 0:1],
+                bias=affine[:, tile_no, 1:2],
+                accum_out=half_sums[:, half : half + 1],
+            )
+        nc.scalar.activation(
+            out=inv_norm[last][:, second], in_=half_sums[:, 0:1], func=ACT.Abs_reciprocal_sqrt, bias=half_sums[:, 1:2]
+        )
+        score(last - 2, 1)
+        for j in range(TILES):
+            score(last - 1, j)
+        fold_norm(last, second)
+        nc.vector.tensor_scalar(
+            out=rows[last][:, 1, HALVES[0]], in0=acc[(last, 1, 0)][:],
+            scalar1=fit[last][:, 1, 0:1], scalar2=fit[last][:, 1, 1:2], op0=ALU.mult, op1=ALU.add,
+        )
+        nc.scalar.activation(
+            out=rows[last][:, 1, HALVES[1]], in_=acc[(last, 1, 1)][:],
+            func=ACT.Identity, scale=fit[last][:, 1, 0:1], bias=fit[last][:, 1, 1:2],
+        )
+        scale_scores(last - 2, 1, nc.scalar)
+        turn_rows(last, on_vector, first, acc_psum)
+        quantise_rows(last, first)
+        turn_rows(last, on_vector, second, acc_psum)
+        score(last, 0)
+        scale_scores(last - 1, 0, nc.scalar)
+        quantise_rows(last, second)
+        scale_scores(last - 1, 1, nc.vector)
+        scale_scores(last, 0, nc.scalar)
+        for half in range(2):
+            score_half(last, 1, half)
+        scale_half(last, 1, 0, nc.vector)
+        scale_half(last, 1, 1, nc.scalar)

from contextlib import ExitStack
import math

import concourse.mybir as mybir
from concourse.masks import make_identity

F32 = mybir.dt.float32
BF16 = mybir.dt.bfloat16
U32 = mybir.dt.uint32
U8 = mybir.dt.uint8
FP8X4 = mybir.dt.float8_e4m3fn_x4
ACT = mybir.ActivationFunctionType
ALU = mybir.AluOpType

P = 128
WORD = 4
PAIR = 2
K_PASS = P * WORD

C = 2048
N = 512
HEADS = 4
DH = C // HEADS
PASSES = C // K_PASS
TILES = 2
ROUNDS_PER_SIDE = C // (TILES * P)
ROUNDS = 2 * ROUNDS_PER_SIDE
ROUNDS_PER_HEAD = DH // (TILES * P)
W_BUFS = 4

WARM_BEFORE_WEIGHTS = 6
WARM_BEFORE_X = 3

BN_SCALE = 1.0 / math.sqrt(1.0 + 1e-5)
MAX_INV_NORM = 1e12
SCALE_PAD = 128
X_STEPS = 2 * PASSES
X_STEP_COLS = N // 2
ALL_TILES = slice(0, TILES)
ONE_TILE = [slice(j, j + 1) for j in range(TILES)]
ALL_PIXELS = slice(0, N)
ALL_SCORES = slice(0, DH)
HALVES = (slice(0, N // 2), slice(N // 2, N))

FLOPS = 2 * 2 * C * C * N + HEADS * 2 * DH * DH * N


def tile_transposedattention_fusion_pa_kernel(
    tc, x1, x2, k_w, k_b, q_w, q_b, temperature, bnk_w, bnk_b, bnq_w, bnq_b, out
):
    nc = tc.nc

    x_views = [
        x.rearrange("b c h w -> (b c) (h w)").rearrange(
            "(g u p e) n -> g p u (e n)", g=PASSES, u=PAIR, p=P, e=PAIR
        )
        for x in (x1, x2)
    ]
    w_views = [w.rearrange("(r j p) c -> r p j c", j=TILES, p=P) for w in (k_w, q_w)]
    out_view = out.rearrange("b h (t p) d -> (b h t) p d", p=P)

    with ExitStack() as ctx:
        const = ctx.enter_context(tc.tile_pool(name="const", bufs=1))
        x_raw_pool = ctx.enter_context(tc.tile_pool(name="x_raw", bufs=2 * PASSES))
        x_grp_pool = ctx.enter_context(tc.tile_pool(name="x_grp", bufs=X_STEPS))
        w_raw_pool = ctx.enter_context(tc.tile_pool(name="w_raw", bufs=W_BUFS))
        w_grp_pool = ctx.enter_context(tc.tile_pool(name="w_grp", bufs=2))
        w_mx_pool = ctx.enter_context(tc.tile_pool(name="w_mx", bufs=3))
        small = ctx.enter_context(tc.tile_pool(name="small", bufs=3))
        rows_pool = ctx.enter_context(tc.tile_pool(name="rows", bufs=3))
        q_mx_pool = ctx.enter_context(tc.tile_pool(name="q_mx", bufs=3))
        out_pool = ctx.enter_context(tc.tile_pool(name="out", bufs=8))
        bank_psum = ctx.enter_context(tc.psum_pool(name="bank", bufs=5))
        acc_psum = ctx.enter_context(tc.psum_pool(name="acc", bufs=3))
        ctx.enter_context(tc.manual_schedule())

        ident = const.tile([P, P], F32, name="ident")
        ident_bf = const.tile([P, P], BF16, name="ident_bf")
        vec_rows = [const.tile([P, P], BF16, name=f"vec_rows_{side}") for side in range(2)]
        vec_cols = const.tile([P, 2, P], F32, name="vec_cols")
        affine = const.tile([P, 2 * C // P, 2], F32, name="affine")
        temp_bf = const.tile([P, HEADS], BF16, name="temp_bf")
        temp = const.tile([P, HEADS], F32, name="temp")
        one = const.tile([P, 1], F32, name="one")
        one_root = const.tile([P, 1], F32, name="one_root")
        warm = const.tile([P, N], BF16, name="warm")
        x_codes = const.tile([P, 2, PASSES, N], U32, name="x_codes", align_bytes=256)
        x_scales_padded = const.tile(
            [P, SCALE_PAD + 2 * PASSES * N], U8, name="x_scales", align_bytes=256
        )
        x_scales = x_scales_padded[:, SCALE_PAD:].rearrange("p (s g n) -> p s g n", s=2, g=PASSES)
        kn_codes = const.tile([P, HEADS, DH], U32, name="kn_codes", align_bytes=64)
        kn_scales = const.tile([P, HEADS, DH], U8, name="kn_scales", align_bytes=64)

        x_raw, x_grp = {}, {}
        w_raw, w_grp, w_codes, w_scales = {}, {}, {}, {}
        acc, sumsq, inv_norm, fit, rows, rows_grp = {}, {}, {}, {}, {}, {}
        qn_codes, qn_scales, scores = {}, {}, {}

        def in_range(r):
            return 0 <= r < ROUNDS

        def load_x(side, g):
            raw = x_raw_pool.tile([P, WORD, N], BF16, name="x_raw", tag="x_raw")
            nc.sync.dma_start(
                out=raw[:].rearrange("p (u e) n -> p u (e n)", u=PAIR), in_=x_views[side][g]
            )
            x_raw[(side, g)] = raw

        def load_w(r, tiles=ALL_TILES):
            if not in_range(r):
                return
            side, part = divmod(r, ROUNDS_PER_SIDE)
            if tiles.start == 0:
                w_raw[r] = w_raw_pool.tile([P, TILES, C], BF16, name="w_raw", tag="w_raw")
            nc.sync.dma_start(out=w_raw[r][:, tiles, :], in_=w_views[side][part][:, tiles, :])

        def regroup_x(side, k, copy):
            if not 0 <= k < X_STEPS:
                return
            g, half = divmod(k, 2)
            cols = slice(half * X_STEP_COLS, (half + 1) * X_STEP_COLS)
            grp = x_grp_pool.tile(
                [P, X_STEP_COLS, WORD], BF16, name="x_grp", tag="x_grp", align_bytes=64
            )
            copy(
                out=grp[:].rearrange("p (c i) t -> p c t i", i=4),
                in_=x_raw[(side, g)][:, :, cols].rearrange("p t (c i) -> p c t i", i=4),
            )
            x_grp[(side, k)] = grp

        def quantise_x(side, k):
            if not 0 <= k < X_STEPS:
                return
            g, half = divmod(k, 2)
            cols = slice(half * X_STEP_COLS, (half + 1) * X_STEP_COLS)
            nc.vector.quantize_mx(
                out=x_codes[:, side, g, cols].bitcast(FP8X4),
                scales=x_scales[:, side, g, cols],
                in_=x_grp[(side, k)][:].rearrange("p n t -> p (n t)"),
            )

        def turn(sources, pool=None):
            tag = "bank" if pool is None else "acc"
            bank = (pool or bank_psum).tile([P, len(sources), PAIR, P], F32, name="bank", tag=tag)
            for a, source in enumerate(sources):
                for u in range(PAIR):
                    nc.tensor.transpose(
                        out=bank[:, a, u, :], in_=source[:, u * P : (u + 1) * P], identity=ident[:]
                    )
            return bank

        def copy_out(bank, dest, copy):
            copy(out=dest, in_=bank[:].rearrange("p a u o -> p a o u"))

        def open_weights(r):
            if not in_range(r):
                return
            w_grp[r] = w_grp_pool.tile(
                [P, TILES, PASSES, P, WORD], BF16, name="w_grp", tag="w_grp", align_bytes=64
            )
            w_codes[r] = w_mx_pool.tile(
                [P, TILES, PASSES, P], U32, name="w_codes", tag="w_codes", align_bytes=64
            )
            w_scales[r] = w_mx_pool.tile(
                [P, TILES, PASSES, P], U8, name="w_scales", tag="w_scales", align_bytes=64
            )

        def turn_weights_in(r, b):
            j, half = divmod(b, 2)
            words = w_raw[r][:].bitcast(F32)
            per_pass = K_PASS // PAIR
            return turn(
                [
                    words[:, j, (2 * half + a) * per_pass : (2 * half + a + 1) * per_pass]
                    for a in range(2)
                ]
            )

        def turn_weights_out(r, b, bank, copy):
            j, half = divmod(b, 2)
            copy_out(bank, w_grp[r][:].bitcast(F32)[:, j, 2 * half : 2 * half + 2, :, :], copy)

        def turn_weights(r, b, copy):
            if in_range(r):
                turn_weights_out(r, b, turn_weights_in(r, b), copy)

        def quantise_weights(r, j):
            if not in_range(r):
                return
            nc.vector.quantize_mx(
                out=w_codes[r][:, j, :, :].rearrange("p g o -> p (g o)").bitcast(FP8X4),
                scales=w_scales[r][:, j, :, :].rearrange("p g o -> p (g o)"),
                in_=w_grp[r][:, j, :, :, :].rearrange("p g o t -> p (g o t)"),
            )

        def project_pass(r, j, g):
            side = r // ROUNDS_PER_SIDE
            if g == 0:
                acc[(r, j)] = acc_psum.tile([P, N], F32, name="acc", tag="acc")
            nc.tensor.matmul_mx(
                out=acc[(r, j)][:],
                lhsT=w_codes[r][:, j, g, :].bitcast(FP8X4),
                lhsT_scale=w_scales[r][:, j, g, :],
                rhs=x_codes[:, side, g, :].bitcast(FP8X4),
                rhs_scale=x_scales[:, side, g, :],
                start=(g == 0),
                stop=(g == PASSES - 1),
            )

        def project(r, j):
            if not in_range(r):
                return
            for g in range(PASSES):
                project_pass(r, j, g)

        def project_half(r, j, half):
            side = r // ROUNDS_PER_SIDE
            cols = HALVES[half]
            acc[(r, j, half)] = acc_psum.tile([P, N // 2], F32, name="acc_half", tag="acc")
            for g in range(PASSES):
                nc.tensor.matmul_mx(
                    out=acc[(r, j, half)][:],
                    lhsT=w_codes[r][:, j, g, :].bitcast(FP8X4),
                    lhsT_scale=w_scales[r][:, j, g, :],
                    rhs=x_codes[:, side, g, cols].bitcast(FP8X4),
                    rhs_scale=x_scales[:, side, g, cols],
                    start=(g == 0),
                    stop=(g == PASSES - 1),
                )

        def square_sum(r, j):
            if not in_range(r):
                return
            if j == 0:
                sumsq[r] = small.tile([P, TILES], F32, name="sumsq", tag="sumsq")
            squares = rows_pool.tile([P, N], BF16, name="squares", tag="squares")
            tile_no = TILES * r + j
            nc.scalar.activation(
                out=squares[:],
                in_=acc[(r, j)][:],
                func=ACT.Square,
                scale=affine[:, tile_no, 0:1],
                bias=affine[:, tile_no, 1:2],
                accum_out=sumsq[r][:, j : j + 1],
            )

        def inverse_norm(r, tiles=ALL_TILES):
            if not in_range(r):
                return
            if tiles.start == 0:
                inv_norm[r] = small.tile([P, TILES], F32, name="inv_norm", tag="inv_norm")
            nc.scalar.activation(
                out=inv_norm[r][:, tiles], in_=sumsq[r][:, tiles], func=ACT.Abs_reciprocal_sqrt
            )

        def fold_norm(r, tiles=ALL_TILES):
            if not in_range(r):
                return
            if tiles.start == 0:
                fit[r] = small.tile([P, TILES, 2], F32, name="fit", tag="fit")
                rows[r] = rows_pool.tile([P, TILES, N], BF16, name="rows", tag="rows")
            count = tiles.stop - tiles.start
            nc.vector.scalar_tensor_tensor(
                out=fit[r][:, tiles, :],
                in0=inv_norm[r][:, tiles].unsqueeze(2).to_broadcast([P, count, 2]),
                scalar=MAX_INV_NORM,
                in1=affine[:, TILES * r + tiles.start : TILES * r + tiles.stop, :],
                op0=ALU.min,
                op1=ALU.mult,
            )

        def normalise_on_vector(r, j, cols=ALL_PIXELS):
            nc.vector.tensor_scalar(
                out=rows[r][:, j, cols],
                in0=acc[(r, j)][:, cols],
                scalar1=fit[r][:, j, 0:1],
                scalar2=fit[r][:, j, 1:2],
                op0=ALU.mult,
                op1=ALU.add,
            )

        def normalise_on_scalar(r, j, cols=ALL_PIXELS):
            nc.scalar.activation(
                out=rows[r][:, j, cols],
                in_=acc[(r, j)][:, cols],
                func=ACT.Identity,
                scale=fit[r][:, j, 0:1],
                bias=fit[r][:, j, 1:2],
            )

        def normalise(r):
            if not in_range(r):
                return
            normalise_on_vector(r, 0)
            normalise_on_scalar(r, 1)

        def open_rows(r):
            rows_grp[r] = rows_pool.tile(
                [P, TILES, P, WORD], BF16, name="rows_grp", tag="rows_grp", align_bytes=64
            )

        def turn_rows(r, copy, tiles=ALL_TILES, pool=None):
            if not in_range(r):
                return
            if tiles.start == 0:
                open_rows(r)
            words = rows[r][:].bitcast(F32)
            bank = turn([words[:, j, :] for j in range(tiles.start, tiles.stop)], pool)
            copy_out(bank, rows_grp[r][:].bitcast(F32)[:, tiles, :, :], copy)

        def quantise_rows(r, tiles=ALL_TILES):
            if not in_range(r):
                return
            side, part = divmod(r, ROUNDS_PER_SIDE)
            head, half = divmod(part, ROUNDS_PER_HEAD)
            width = TILES * P
            if side == 0:
                codes = kn_codes[:, head, half * width : (half + 1) * width]
                scales = kn_scales[:, head, half * width : (half + 1) * width]
            else:
                if tiles.start == 0:
                    qn_codes[r] = q_mx_pool.tile([P, width], U32, name="qn_codes", tag="qn_codes", align_bytes=64)
                    qn_scales[r] = q_mx_pool.tile([P, width], U8, name="qn_scales", tag="qn_scales", align_bytes=64)
                codes, scales = qn_codes[r][:], qn_scales[r][:]
            cols = slice(tiles.start * P, tiles.stop * P)
            nc.vector.quantize_mx(
                out=codes[:, cols].bitcast(FP8X4),
                scales=scales[:, cols],
                in_=rows_grp[r][:, tiles, :, :].rearrange("p j o t -> p (j o t)"),
            )

        def score(r, j):
            if not ROUNDS_PER_SIDE <= r < ROUNDS:
                return
            part = r - ROUNDS_PER_SIDE
            head = part // ROUNDS_PER_HEAD
            bank = bank_psum.tile([P, DH], F32, name="score", tag="bank")
            nc.tensor.matmul_mx(
                out=bank[:],
                lhsT=qn_codes[r][:, j * P : (j + 1) * P].bitcast(FP8X4),
                lhsT_scale=qn_scales[r][:, j * P : (j + 1) * P],
                rhs=kn_codes[:, head, :].bitcast(FP8X4),
                rhs_scale=kn_scales[:, head, :],
                start=True,
                stop=True,
            )
            scores[(r, j)] = bank

        def scale_scores(r, j, engine, cols=ALL_SCORES):
            if not ROUNDS_PER_SIDE <= r < ROUNDS:
                return
            part = r - ROUNDS_PER_SIDE
            factor = temp[:, part // ROUNDS_PER_HEAD : part // ROUNDS_PER_HEAD + 1]
            bank = scores[(r, j)]
            result = out_pool.tile([P, cols.stop - cols.start], F32, name="result", tag="result")
            if engine is nc.scalar:
                nc.scalar.activation(out=result[:], in_=bank[:, cols], func=ACT.Copy, scale=factor)
            else:
                nc.vector.tensor_scalar(
                    out=result[:], in0=bank[:, cols], scalar1=factor, scalar2=None, op0=ALU.mult
                )
            nc.sync.dma_start(out=out_view[TILES * part + j][:, cols], in_=result[:])

        def score_half(r, j, half):
            head = (r - ROUNDS_PER_SIDE) // ROUNDS_PER_HEAD
            bank = bank_psum.tile([P, DH // 2], F32, name="score_half", tag="bank")
            nc.tensor.matmul_mx(
                out=bank[:],
                lhsT=qn_codes[r][:, j * P : (j + 1) * P].bitcast(FP8X4),
                lhsT_scale=qn_scales[r][:, j * P : (j + 1) * P],
                rhs=kn_codes[:, head, HALVES[half]].bitcast(FP8X4),
                rhs_scale=kn_scales[:, head, HALVES[half]],
                start=True,
                stop=True,
            )
            scores[(r, j, half)] = bank

        def scale_half(r, j, half, engine):
            part = r - ROUNDS_PER_SIDE
            factor = temp[:, part // ROUNDS_PER_HEAD : part // ROUNDS_PER_HEAD + 1]
            bank = scores[(r, j, half)]
            result = out_pool.tile([P, DH // 2], F32, name="result", tag="result")
            if engine is nc.scalar:
                nc.scalar.activation(out=result[:], in_=bank[:], func=ACT.Copy, scale=factor)
            else:
                nc.vector.tensor_scalar(out=result[:], in0=bank[:], scalar1=factor, scalar2=None, op0=ALU.mult)
            nc.sync.dma_start(out=out_view[TILES * part + j][:, HALVES[half]], in_=result[:])

        def x2_steps(r):
            return range(3 * (r - 2) // 2, 3 * (r - 1) // 2) if 2 <= r < ROUNDS_PER_SIDE else ()

        def iteration(r):
            quantise_weights(r, 1)
            if r > 1:
                inverse_norm(r - 1)
            turn_rows(r - 2, nc.vector.tensor_copy)
            open_weights(r + 1)
            turn_weights(r + 1, 0, nc.scalar.copy)
            turn_weights(r + 1, 1, nc.scalar.copy)
            if r > 1:
                fold_norm(r - 1)
            x2_ready = x2_steps(r - 1)
            for k in x2_ready:
                quantise_x(1, k)
            if not x2_ready:
                quantise_rows(r - 2)
            if r > 1:
                normalise_on_vector(r - 1, 0)
            if x2_ready:
                quantise_rows(r - 2)
            helped = 1 < r < ROUNDS_PER_SIDE
            turn_weights(r + 1, 2, nc.scalar.copy if helped else nc.vector.tensor_copy)
            turn_weights(r + 1, 3, nc.scalar.copy)
            if r > 1:
                normalise_on_scalar(r - 1, 1)
            load_w(r + 1 + W_BUFS)
            if r == 1:
                load_x(1, 3)
            for j in range(TILES):
                score(r - 3, j)
                scale_scores(r - 3, j, (nc.scalar, nc.vector)[j])
            quantise_weights(r + 1, 0)
            for k in x2_steps(r):
                regroup_x(1, k, nc.vector.tensor_copy)
            for j in range(TILES):
                project(r, j)
                square_sum(r, j)

        rows_per_vec = C // P
        vec_bank = {}

        def load_vectors(side):
            for v, vec in enumerate(((k_b, bnk_w, bnk_b), (q_b, bnq_w, bnq_b))[side]):
                nc.sync.dma_start(
                    out=vec_rows[side][v * rows_per_vec : (v + 1) * rows_per_vec, :],
                    in_=vec.rearrange("(i p) -> i p", p=P),
                )

        def turn_vectors(side):
            vec_bank[side] = bank_psum.tile([P, P], BF16, name="vec_bank", tag="bank")
            nc.tensor.transpose(out=vec_bank[side][:], in_=vec_rows[side][:], identity=ident_bf[:])

        def make_affine(side):
            cols = vec_cols[:, side, :]
            nc.scalar.copy(out=cols, in_=vec_bank[side][:])
            bias, bn_w, bn_b = [cols[:, v * rows_per_vec : (v + 1) * rows_per_vec] for v in range(3)]
            mine = affine[:, side * rows_per_vec : (side + 1) * rows_per_vec, :]
            gain, shift = mine[:, :, 0], mine[:, :, 1]
            nc.gpsimd.tensor_scalar(out=gain, in0=bn_w, scalar1=BN_SCALE, scalar2=None, op0=ALU.mult)
            nc.gpsimd.tensor_tensor(out=shift, in0=bias, in1=gain, op=ALU.mult)
            nc.gpsimd.tensor_tensor(out=shift, in0=shift, in1=bn_b, op=ALU.add)

        nc.vector.memset(warm[:], 0.0)
        nc.vector.memset(one[:], 1.0)
        for side in range(2):
            nc.gpsimd.memset(vec_rows[side][:], 0.0)
        nc.scalar.activation(out=one_root[:], in_=one[:], func=ACT.Abs_reciprocal_sqrt)
        make_identity(nc, ident_bf[:])
        make_identity(nc, ident[:])

        load_x(0, 0)
        load_w(0, ONE_TILE[0])
        load_x(0, 1)
        load_w(0, ONE_TILE[1])
        load_x(0, 2)
        load_vectors(0)
        load_x(0, 3)
        for r in (1, 2):
            for tile in ONE_TILE:
                load_w(r, tile)
        load_vectors(1)
        nc.sync.dma_start(
            out=temp_bf[:], in_=temperature.rearrange("h a b -> (h a b)").partition_broadcast(P)
        )
        load_x(1, 0)
        load_w(W_BUFS - 1)

        warm_bank = acc_psum.tile([P, N], F32, name="warm_bank", tag="acc")

        def warm_up(count):
            for n in range(count):
                nc.tensor.matmul(out=warm_bank[:], lhsT=warm[:, 0:P], rhs=warm[:], start=True, stop=True)

        warm_up(WARM_BEFORE_WEIGHTS)
        open_weights(0)
        open_weights(1)
        regroup_x(0, 0, nc.vector.tensor_copy)
        regroup_x(0, 1, nc.scalar.copy)
        quantise_x(0, 0)
        quantise_x(0, 1)
        turn_weights(0, 0, nc.scalar.copy)
        turn_weights(0, 1, nc.vector.tensor_copy)
        warm_up(WARM_BEFORE_X)
        regroup_x(0, 2, nc.vector.tensor_copy)
        regroup_x(0, 3, nc.scalar.copy)
        quantise_weights(0, 0)
        turn_weights(0, 2, nc.scalar.copy)
        turn_weights(0, 3, nc.scalar.copy)
        load_w(W_BUFS)
        load_x(1, 1)
        quantise_x(0, 2)
        quantise_x(0, 3)
        for g in range(2):
            project_pass(0, 0, g)
        regroup_x(0, 4, nc.vector.tensor_copy)
        regroup_x(0, 5, nc.scalar.copy)
        quantise_weights(0, 1)
        for g in range(2):
            project_pass(0, 1, g)
        turn_vectors(0)
        quantise_x(0, 4)
        regroup_x(0, 6, nc.vector.tensor_copy)
        regroup_x(0, 7, nc.scalar.copy)
        quantise_x(0, 5)
        w1_banks = [turn_weights_in(1, b) for b in range(2)]
        for j in range(TILES):
            project_pass(0, j, 2)
        quantise_x(0, 6)
        quantise_x(0, 7)
        make_affine(0)
        turn_weights_out(1, 0, w1_banks[0], nc.scalar.copy)
        for j in range(TILES):
            project_pass(0, j, 3)
        turn_weights_out(1, 1, w1_banks[1], nc.vector.tensor_copy)
        square_sum(0, 0)
        turn_weights(1, 2, nc.vector.tensor_copy)
        square_sum(0, 1)
        inverse_norm(0)
        quantise_weights(1, 0)
        turn_weights(1, 3, nc.scalar.copy)
        fold_norm(0)
        normalise(0)
        load_w(1 + W_BUFS)
        load_x(1, 2)

        for r in range(1, ROUNDS - 1):
            iteration(r)
            if r == 1:
                turn_vectors(1)
                make_affine(1)
                nc.vector.tensor_copy(out=temp[:], in_=temp_bf[:])

        last = ROUNDS - 1
        first, second = ONE_TILE
        on_vector, on_scalar = nc.vector.tensor_copy, nc.scalar.copy
        quantise_weights(last, 1)
        inverse_norm(last - 1)
        turn_rows(last - 2, on_vector)
        fold_norm(last - 1)
        quantise_rows(last - 2)
        normalise(last - 1)
        for j in range(TILES):
            score(last - 3, j)
        scale_scores(last - 3, 0, nc.scalar)
        project(last, 0)
        score(last - 2, 0)
        square_sum(last, 0)
        scale_scores(last - 3, 1, nc.vector)
        inverse_norm(last, first)
        turn_rows(last - 1, on_vector)
        for half in range(2):
            project_half(last, 1, half)
        fold_norm(last, first)
        scale_scores(last - 2, 0, nc.scalar)
        quantise_rows(last - 1)
        normalise_on_vector(last, 0)
        half_sums = small.tile([P, 2], F32, name="half_sums")
        tile_no = TILES * last + 1
        for half in range(2):
            squares = rows_pool.tile([P, N], BF16, name="squares", tag="squares")
            nc.scalar.activation(
                out=squares[:, HALVES[half]],
                in_=acc[(last, 1, half)][:],
                func=ACT.Square,
                scale=affine[:, tile_no, 0:1],
                bias=affine[:, tile_no, 1:2],
                accum_out=half_sums[:, half : half + 1],
            )
        nc.scalar.activation(
            out=inv_norm[last][:, second], in_=half_sums[:, 0:1], func=ACT.Abs_reciprocal_sqrt, bias=half_sums[:, 1:2]
        )
        score(last - 2, 1)
        for j in range(TILES):
            score(last - 1, j)
        fold_norm(last, second)
        nc.vector.tensor_scalar(
            out=rows[last][:, 1, HALVES[0]], in0=acc[(last, 1, 0)][:],
            scalar1=fit[last][:, 1, 0:1], scalar2=fit[last][:, 1, 1:2], op0=ALU.mult, op1=ALU.add,
        )
        nc.scalar.activation(
            out=rows[last][:, 1, HALVES[1]], in_=acc[(last, 1, 1)][:],
            func=ACT.Identity, scale=fit[last][:, 1, 0:1], bias=fit[last][:, 1, 1:2],
        )
        scale_scores(last - 2, 1, nc.scalar)
        turn_rows(last, on_vector, first, acc_psum)
        quantise_rows(last, first)
        turn_rows(last, on_vector, second, acc_psum)
        score(last, 0)
        scale_scores(last - 1, 0, nc.scalar)
        quantise_rows(last, second)
        scale_scores(last - 1, 1, nc.vector)
        scale_scores(last, 0, nc.scalar)
        for half in range(2):
            score_half(last, 1, half)
        scale_half(last, 1, 0, nc.vector)
        scale_half(last, 1, 1, nc.scalar)
